import numpy as np
import ml_dtypes


def mxq(x, axis, fmt="e4m3"):
    dtype, down = {"e4m3": (ml_dtypes.float8_e4m3fn, 7), "e5m2": (ml_dtypes.float8_e5m2, 14)}[fmt]
    v = np.moveaxis(np.asarray(x, np.float32).astype(ml_dtypes.bfloat16).astype(np.float64), axis, -1)
    blocks = v.reshape(v.shape[:-1] + (-1, 32))
    amax = np.abs(blocks).max(-1, keepdims=True)
    byte = np.maximum(np.where(amax > 0, np.frexp(amax)[1] - 1 + 127, 0) - down, 1)
    scale = np.exp2(byte - 127.0)
    codes = (blocks / scale).astype(np.float32).astype(dtype).astype(np.float64)
    return np.moveaxis((codes * scale).reshape(v.shape), -1, axis)


WIDE = False


def mx_kscale(k):
    if not WIDE:
        return np.ones(k)
    levels = np.array([10, -10, 5, -5, 0])
    a = np.random.permutation(np.resize(levels, k // 512 * 4)).reshape(k // 512, 4)
    idx = np.arange(k)
    return np.exp2(a[idx // 512, idx % 128 // 32])


BF16 = ml_dtypes.bfloat16


def bf(x):
    return np.asarray(x, np.float32).astype(BF16)


def f64(x):
    return np.asarray(x).astype(np.float64)


B, S, A, D, V, KS, KM, KF = 4, 64, 16, 1024, 4096, 1024, 512, 512


def erf(v):
    z = np.clip(v, -6.0, 6.0)
    zz = 2.0 * z * z
    term = z.copy()
    total = z.copy()
    for n in range(1, 120):
        term = term * zz / (2.0 * n + 1.0)
        total = total + term
    return 2.0 / np.sqrt(np.pi) * np.exp(-z * z) * total


def gelu(v):
    return 0.5 * v * (1.0 + erf(v / np.sqrt(2.0)))


def sigmoid(v):
    return 1.0 / (1.0 + np.exp(-v))


def setup_inputs():
    s = mx_kscale(D)
    rn = np.random.standard_normal
    return {"hidden_states": bf(rn((B, S, D)) * s),
            "logits": bf(rn((B, S, V))),
            "W_f1": bf(rn((D, KF)) / np.sqrt(D) / s[:, None]),
            "b_f1": bf(rn(KF) * 0.5),
            "W_f2": bf(rn((KF, V)) * 2.5 / np.sqrt(KF)),
            "b_f2": bf(rn(V) * 0.5)}


def reference(hidden_states, logits, W_f1, b_f1, W_f2, b_f2):
    hid_f = gelu((mxq(f64(hidden_states), 2, "e4m3") @ mxq(f64(W_f1), 0, "e4m3")) + f64(b_f1))
    focus = sigmoid((mxq(hid_f, 2, "e4m3") @ mxq(f64(W_f2), 0, "e4m3")) + f64(b_f2))
    return f64(logits) * (1.0 + focus)

@@ -1,0 +1,327 @@
+from contextlib import ExitStack
+
+import concourse.mybir as mybir
+from concourse.masks import make_identity
+
+F32 = mybir.dt.float32
+BF16 = mybir.dt.bfloat16
+I32 = mybir.dt.int32
+U32 = mybir.dt.uint32
+U8 = mybir.dt.uint8
+FP8X4 = mybir.dt.float8_e4m3fn_x4
+ACT = mybir.ActivationFunctionType
+ALU = mybir.AluOpType
+
+P = 128
+TOK = 256
+D_IN = 1024
+D_HID = 512
+VOC = 4096
+CH = 512
+NCH = VOC // CH
+FLOPS = 2 * TOK * D_IN * D_HID + 2 * TOK * D_HID * VOC
+
+W1_VEC = 320
+W2_VEC = [256,256,256,256,256,256,256,256]
+W2_LOADS = [[0,1],[1,2],[2,4],[4,6],[6,8]]
+LG_LOADS = [[0,4],[4,8]]
+LOAD_ORDER = ["g0","h0","g1","w0","w1","w2","l0","w3","w4","l1"]
+
+
+def regroup(engine_copy, dst, src, c0, c1, s0):
+    engine_copy(
+        out=dst[:, c0:c1, :].rearrange("p (c i) t -> p c t i", i=4),
+        in_=src[:, :, s0 + c0 : s0 + c1].rearrange("p t (c i) -> p c t i", i=4),
+    )
+
+
+def tile_sparseoutputprojection_pb_kernel(tc, hidden_states, logits, W_f1, b_f1, W_f2, b_f2, out):
+    nc = tc.nc
+    with ExitStack() as ctx:
+        keep = ctx.enter_context(tc.tile_pool(name="keep", bufs=1))
+        ring = ctx.enter_context(tc.tile_pool(name="ring", bufs=3))
+        psum = ctx.enter_context(tc.psum_pool(name="psum", bufs=4))
+
+        h_dram = hidden_states.flatten_outer_dims().rearrange("(a p) k -> p a k", p=P)
+        lg_dram = logits.flatten_outer_dims().rearrange("(a p) v -> p a v", p=P)
+        out_dram = out.flatten_outer_dims().rearrange("(a p) v -> p a v", p=P)
+        w2_dram = W_f2.rearrange("(t p) v -> p t v", p=P)
+
+        braw = keep.tile([P, P], BF16, name="braw")
+        nc.vector.memset(braw[:].bitcast(I32), 0)
+        warm = keep.tile([P, 1], F32, name="warm")
+        nc.vector.memset(warm[:], 0.0)
+        ident = keep.tile([P, P], F32, name="ident")
+        make_identity(nc, ident[:])
+        nc.scalar.dma_start(out=braw[0:32, :], in_=b_f2.rearrange("(j p) -> j p", p=P))
+        nc.scalar.dma_start(out=braw[32:36, :], in_=b_f1.rearrange("(j p) -> j p", p=P))
+        warm_g = keep.tile([P, 1], F32, name="warm_g")
+        nc.scalar.activation(out=warm_g[:], in_=warm[:], func=ACT.Gelu)
+
+        h_sb = keep.tile([P, 2, D_IN], BF16, name="h_sb")
+        w1raw = [keep.tile([P, 4, D_HID], BF16, name="w1raw%d" % g) for g in range(2)]
+        w2raw = [keep.tile([P, 4, (b - a) * CH], BF16, name="w2raw%d" % i) for i, (a, b) in enumerate(W2_LOADS)]
+        lg_sb = [keep.tile([P, 2, (b - a) * CH], BF16, name="lg%d" % i) for i, (a, b) in enumerate(LG_LOADS)]
+        for item in LOAD_ORDER:
+            kind, idx = item[0], int(item[1:])
+            if kind == "h":
+                nc.sync.dma_start(out=h_sb[:], in_=h_dram)
+            elif kind == "g":
+                nc.sync.dma_start(
+                    out=w1raw[idx][:].rearrange("p (u e) f -> p u e f", u=2),
+                    in_=W_f1[idx * 512 : (idx + 1) * 512, :].rearrange("(u p e) f -> p u e f", u=2, p=P, e=2),
+                )
+            elif kind == "w":
+                a, b = W2_LOADS[idx]
+                nc.sync.dma_start(out=w2raw[idx][:], in_=w2_dram[:, :, a * CH : b * CH])
+            else:
+                a, b = LG_LOADS[idx]
+                nc.sync.dma_start(out=lg_sb[idx][:], in_=lg_dram[:, :, a * CH : b * CH])
+
+        def w2_src(c):
+            for i, (a, b) in enumerate(W2_LOADS):
+                if a <= c < b:
+                    return w2raw[i], (c - a) * CH
+            raise ValueError("chunk")
+
+        def lg_src(c):
+            for i, (a, b) in enumerate(LG_LOADS):
+                if a <= c < b:
+                    return lg_sb[i], (c - a) * CH
+            raise ValueError("chunk")
+
+        bf32 = keep.tile([P, P], F32, name="bf32")
+        bias = keep.tile([P, 36], F32, name="bias")
+        hgrp = keep.tile([P, 2 * TOK * 4], BF16, name="hgrp", align_bytes=64)
+        hcodes = keep.tile([P, 2 * TOK], U32, name="hcodes", align_bytes=64)
+        hscales = keep.tile([P, 2 * TOK], U8, name="hscales", align_bytes=64)
+        w1grp = [keep.tile([P, D_HID, 4], BF16, name="w1grp%d" % g, align_bytes=64) for g in range(2)]
+        w1codes = keep.tile([P, 2 * D_HID], U32, name="w1codes", align_bytes=64)
+        w1scales = keep.tile([P, 2 * D_HID], U8, name="w1scales", align_bytes=64)
+        hidp = keep.tile([P, 4, TOK], BF16, name="hidp")
+        hidg = keep.tile([P, TOK, 4], BF16, name="hidg", align_bytes=64)
+        hidcodes = keep.tile([P, TOK], U32, name="hidcodes", align_bytes=64)
+        hidscales = keep.tile([P, TOK], U8, name="hidscales", align_bytes=64)
+        w2codes = [keep.tile([P, CH], U32, name="w2codes%d" % c, align_bytes=64) for c in range(NCH)]
+        w2scales = [keep.tile([P, CH], U8, name="w2scales%d" % c, align_bytes=64) for c in range(NCH)]
+        osb = [keep.tile([P, 2, CH], F32, name="osb%d" % c) for c in range(NCH)]
+        state = {}
+
+        def op_bias():
+            nc.vector.tensor_copy(out=bf32[:], in_=braw[:])
+            bt = psum.tile([P, P], F32, tag="ft", name="bt")
+            nc.tensor.transpose(bt[:], bf32[:], ident[:])
+            state["bt"] = bt
+
+        def op_bcopy():
+            nc.vector.tensor_copy(out=bias[:], in_=state["bt"][:, 0:36])
+
+        def op_th():
+            hw = h_sb[:].rearrange("p a k -> p (a k)").bitcast(F32)
+            for g in range(2):
+                xt = psum.tile([P, 2, TOK], F32, tag="ft", name="xt%d" % g)
+                for u in range(2):
+                    for a in range(2):
+                        w0 = a * 512 + (2 * g + u) * P
+                        nc.tensor.transpose(xt[:, u, a * P : (a + 1) * P], hw[:, w0 : w0 + P], ident[:])
+                state["xt%d" % g] = xt
+
+        def op_evh():
+            hv = hgrp[:].bitcast(F32)
+            for g, copy in ((0, nc.vector.tensor_copy), (1, nc.scalar.copy)):
+                copy(
+                    out=hv[:, g * 512 : (g + 1) * 512].rearrange("p (r u) -> p r u", u=2),
+                    in_=state["xt%d" % g][:].rearrange("p u r -> p r u"),
+                )
+
+        def op_a1(g):
+            regroup(nc.vector.tensor_copy, w1grp[g], w1raw[g], 0, W1_VEC, 0)
+            regroup(nc.scalar.copy, w1grp[g], w1raw[g], W1_VEC, D_HID, 0)
+
+        def op_qh():
+            nc.vector.quantize_mx(out=hcodes[:].bitcast(FP8X4), scales=hscales[:], in_=hgrp[:])
+
+        def op_q1(g):
+            cols = slice(g * D_HID, (g + 1) * D_HID)
+            nc.vector.quantize_mx(
+                out=w1codes[:, cols].bitcast(FP8X4),
+                scales=w1scales[:, cols],
+                in_=w1grp[g][:].rearrange("p f t -> p (f t)"),
+            )
+
+        def op_mx1():
+            ps1 = [psum.tile([P, TOK], F32, tag="z", name="ps1_%d" % i) for i in range(4)]
+            for g in range(2):
+                for i in range(4):
+                    wc = slice(g * D_HID + i * P, g * D_HID + (i + 1) * P)
+                    hc = slice(g * TOK, (g + 1) * TOK)
+                    nc.tensor.matmul_mx(
+                        out=ps1[i][:],
+                        lhsT=w1codes[:, wc].bitcast(FP8X4),
+                        lhsT_scale=w1scales[:, wc],
+                        rhs=hcodes[:, hc].bitcast(FP8X4),
+                        rhs_scale=hscales[:, hc],
+                        start=(g == 0),
+                        stop=(g == 1),
+                    )
+            state["ps1"] = ps1
+
+        def op_gelu():
+            for i in range(4):
+                nc.scalar.activation(
+                    out=hidp[:, i, :], in_=state["ps1"][i][:], func=ACT.Gelu, bias=bias[:, 32 + i : 33 + i], scale=1.0
+                )
+            warm_s = keep.tile([P, 1], F32, name="warm_s")
+            nc.scalar.activation(out=warm_s[:], in_=hidp[:, 3, 0:1], func=ACT.Sigmoid)
+
+        def op_hidre():
+            regroup(nc.vector.tensor_copy, hidg, hidp, 0, TOK, 0)
+
+        def op_qhid():
+            nc.vector.quantize_mx(
+                out=hidcodes[:].bitcast(FP8X4), scales=hidscales[:], in_=hidg[:].rearrange("p r t -> p (r t)")
+            )
+
+        def op_a(c):
+            grp = ring.tile([P, CH, 4], BF16, tag="w2grp", name="w2grp%d" % c, align_bytes=64)
+            src, s0 = w2_src(c)
+            if W2_VEC[c] > 0:
+                regroup(nc.vector.tensor_copy, grp, src, 0, W2_VEC[c], s0)
+            if W2_VEC[c] < CH:
+                regroup(nc.scalar.copy, grp, src, W2_VEC[c], CH, s0)
+            state["grp%d" % c] = grp
+
+        def op_b(c):
+            nc.vector.quantize_mx(
+                out=w2codes[c][:].bitcast(FP8X4),
+                scales=w2scales[c][:],
+                in_=state["grp%d" % c][:].rearrange("p v t -> p (v t)"),
+            )
+
+        def op_c(c):
+            zs = [psum.tile([P, 2, TOK], F32, tag="z", name="z%d_%d" % (c, k)) for k in range(2)]
+            for j in range(4):
+                cols = slice(j * P, (j + 1) * P)
+                nc.tensor.matmul_mx(
+                    out=zs[j // 2][:, j % 2, :],
+                    lhsT=w2codes[c][:, cols].bitcast(FP8X4),
+                    lhsT_scale=w2scales[c][:, cols],
+                    rhs=hidcodes[:].bitcast(FP8X4),
+                    rhs_scale=hidscales[:],
+                    start=True,
+                    stop=True,
+                )
+            state["z%d" % c] = zs
+
+        def op_d(c):
+            st = ring.tile([P, 4, TOK], F32, tag="sT", name="sT%d" % c)
+            for j in range(4):
+                nc.scalar.activation(
+                    out=st[:, j, :],
+                    in_=state["z%d" % c][j // 2][:, j % 2, :],
+                    func=ACT.Sigmoid,
+                    bias=bias[:, 4 * c + j : 4 * c + j + 1],
+                    scale=1.0,
+                )
+            state["sT%d" % c] = st
+
+        def op_e(c):
+            fts = []
+            for a in range(2):
+                ft = psum.tile([P, CH], F32, tag="ft", name="ft%d_%d" % (c, a))
+                for j in range(4):
+                    nc.tensor.transpose(ft[:, j * P : (j + 1) * P], state["sT%d" % c][:, j, a * P : (a + 1) * P], ident[:])
+                fts.append(ft)
+            state["ft%d" % c] = fts
+
+        def op_f(c):
+            lg, l0 = lg_src(c)
+            for a in range(2):
+                nc.vector.scalar_tensor_tensor(
+                    out=osb[c][:, a, :],
+                    in0=state["ft%d" % c][a][:],
+                    scalar=1.0,
+                    in1=lg[:, a, l0 : l0 + CH],
+                    op0=ALU.add,
+                    op1=ALU.mult,
+                )
+                if c == NCH - 1:
+                    nc.sync.dma_start(out=out_dram[:, a, c * CH : (c + 1) * CH], in_=osb[c][:, a, :])
+            if c < NCH - 1:
+                nc.sync.dma_start(out=out_dram[:, :, c * CH : (c + 1) * CH], in_=osb[c][:])
+
+        named = {
+            "bias": op_bias, "bcopy": op_bcopy, "Th": op_th, "evh": op_evh, "qh": op_qh,
+            "MX1": op_mx1, "gelu": op_gelu, "hidre": op_hidre, "qhid": op_qhid,
+        }
+        indexed = {"a": op_a1, "q": op_q1, "A": op_a, "B": op_b, "C": op_c, "D": op_d, "E": op_e, "F": op_f}
+        for word in SEQ:
+            if word in named:
+                named[word]()
+            else:
+                indexed[word[0]](int(word[1:]))
+
+
+SEQ = (
+    "bias",
+    "a0",
+    "Th",
+    "evh",
+    "q0",
+    "a1",
+    "bcopy",
+    "qh",
+    "q1",
+    "MX1",
+    "A0",
+    "A1",
+    "B0",
+    "gelu",
+    "A2",
+    "B1",
+    "hidre",
+    "A3",
+    "qhid",
+    "B2",
+    "C0",
+    "C1",
+    "D0",
+    "E0",
+    "A4",
+    "B3",
+    "C2",
+    "D1",
+    "E1",
+    "F0",
+    "A5",
+    "B4",
+    "C3",
+    "D2",
+    "E2",
+    "F1",
+    "A6",
+    "B5",
+    "C4",
+    "D3",
+    "E3",
+    "F2",
+    "A7",
+    "B6",
+    "C5",
+    "D4",
+    "E4",
+    "F3",
+    "B7",
+    "C6",
+    "D5",
+    "E5",
+    "F4",
+    "C7",
+    "D6",
+    "E6",
+    "F5",
+    "D7",
+    "E7",
+    "F6",
+    "F7",
+)

@@ -21,11 +21,13 @@ CH = 512
 NCH = VOC // CH
 FLOPS = 2 * TOK * D_IN * D_HID + 2 * TOK * D_HID * VOC
 
-W1_VEC = 320
-W2_VEC = [256,256,256,256,256,256,256,256]
-W2_LOADS = [[0,1],[1,2],[2,4],[4,6],[6,8]]
+W1_VEC = [320,320]
+W2_VEC = [336,336,336,336,336,336,336,336]
+W2_GPS = [0,0,0,0,0,0,0,0]
+W2_LOADS = [[0,2],[2,4],[4,6],[6,8]]
 LG_LOADS = [[0,4],[4,8]]
-LOAD_ORDER = ["g0","h0","g1","w0","w1","w2","l0","w3","w4","l1"]
+LOAD_ORDER = ["h0","g0","g1","w0","w1","l0","w2","w3","l1"]
+GRP_BUFS = 3
 
 
 def regroup(engine_copy, dst, src, c0, c1, s0):
@@ -38,8 +40,10 @@ def regroup(engine_copy, dst, src, c0, c1, s0):
 def tile_sparseoutputprojection_pb_kernel(tc, hidden_states, logits, W_f1, b_f1, W_f2, b_f2, out):
     nc = tc.nc
     with ExitStack() as ctx:
+        ctx.enter_context(tc.manual_schedule())
         keep = ctx.enter_context(tc.tile_pool(name="keep", bufs=1))
         ring = ctx.enter_context(tc.tile_pool(name="ring", bufs=3))
+        gring = ctx.enter_context(tc.tile_pool(name="gring", bufs=GRP_BUFS))
         psum = ctx.enter_context(tc.psum_pool(name="psum", bufs=4))
 
         h_dram = hidden_states.flatten_outer_dims().rearrange("(a p) k -> p a k", p=P)
@@ -107,8 +111,10 @@ def tile_sparseoutputprojection_pb_kernel(tc, hidden_states, logits, W_f1, b_f1,
         osb = [keep.tile([P, 2, CH], F32, name="osb%d" % c) for c in range(NCH)]
         state = {}
 
-        def op_bias():
+        def op_bcast():
             nc.vector.tensor_copy(out=bf32[:], in_=braw[:])
+
+        def op_tb():
             bt = psum.tile([P, P], F32, tag="ft", name="bt")
             nc.tensor.transpose(bt[:], bf32[:], ident[:])
             state["bt"] = bt
@@ -116,27 +122,27 @@ def tile_sparseoutputprojection_pb_kernel(tc, hidden_states, logits, W_f1, b_f1,
         def op_bcopy():
             nc.vector.tensor_copy(out=bias[:], in_=state["bt"][:, 0:36])
 
-        def op_th():
+        def op_th(g):
             hw = h_sb[:].rearrange("p a k -> p (a k)").bitcast(F32)
-            for g in range(2):
-                xt = psum.tile([P, 2, TOK], F32, tag="ft", name="xt%d" % g)
-                for u in range(2):
-                    for a in range(2):
-                        w0 = a * 512 + (2 * g + u) * P
-                        nc.tensor.transpose(xt[:, u, a * P : (a + 1) * P], hw[:, w0 : w0 + P], ident[:])
-                state["xt%d" % g] = xt
+            xt = psum.tile([P, 2, TOK], F32, tag="ft", name="xt%d" % g)
+            for u in range(2):
+                for a in range(2):
+                    w0 = a * 512 + (2 * g + u) * P
+                    nc.tensor.transpose(xt[:, u, a * P : (a + 1) * P], hw[:, w0 : w0 + P], ident[:])
+            state["xt%d" % g] = xt
 
-        def op_evh():
-            hv = hgrp[:].bitcast(F32)
-            for g, copy in ((0, nc.vector.tensor_copy), (1, nc.scalar.copy)):
-                copy(
-                    out=hv[:, g * 512 : (g + 1) * 512].rearrange("p (r u) -> p r u", u=2),
-                    in_=state["xt%d" % g][:].rearrange("p u r -> p r u"),
-                )
+        def op_evh(g):
+            copy = nc.vector.tensor_copy if g == 0 else nc.scalar.copy
+            copy(
+                out=hgrp[:].bitcast(F32)[:, g * 512 : (g + 1) * 512].rearrange("p (r u) -> p r u", u=2),
+                in_=state["xt%d" % g][:].rearrange("p u r -> p r u"),
+            )
 
-        def op_a1(g):
-            regroup(nc.vector.tensor_copy, w1grp[g], w1raw[g], 0, W1_VEC, 0)
-            regroup(nc.scalar.copy, w1grp[g], w1raw[g], W1_VEC, D_HID, 0)
+        def op_a1v(g):
+            regroup(nc.vector.tensor_copy, w1grp[g], w1raw[g], 0, W1_VEC[g], 0)
+
+        def op_a1s(g):
+            regroup(nc.scalar.copy, w1grp[g], w1raw[g], W1_VEC[g], D_HID, 0)
 
         def op_qh():
             nc.vector.quantize_mx(out=hcodes[:].bitcast(FP8X4), scales=hscales[:], in_=hgrp[:])
@@ -149,28 +155,28 @@ def tile_sparseoutputprojection_pb_kernel(tc, hidden_states, logits, W_f1, b_f1,
                 in_=w1grp[g][:].rearrange("p f t -> p (f t)"),
             )
 
-        def op_mx1():
-            ps1 = [psum.tile([P, TOK], F32, tag="z", name="ps1_%d" % i) for i in range(4)]
-            for g in range(2):
-                for i in range(4):
-                    wc = slice(g * D_HID + i * P, g * D_HID + (i + 1) * P)
-                    hc = slice(g * TOK, (g + 1) * TOK)
-                    nc.tensor.matmul_mx(
-                        out=ps1[i][:],
-                        lhsT=w1codes[:, wc].bitcast(FP8X4),
-                        lhsT_scale=w1scales[:, wc],
-                        rhs=hcodes[:, hc].bitcast(FP8X4),
-                        rhs_scale=hscales[:, hc],
-                        start=(g == 0),
-                        stop=(g == 1),
-                    )
-            state["ps1"] = ps1
-
-        def op_gelu():
+        def op_mx1(g):
+            if g == 0:
+                state["ps1"] = [psum.tile([P, TOK], F32, tag="z", name="ps1_%d" % i) for i in range(4)]
             for i in range(4):
-                nc.scalar.activation(
-                    out=hidp[:, i, :], in_=state["ps1"][i][:], func=ACT.Gelu, bias=bias[:, 32 + i : 33 + i], scale=1.0
+                wc = slice(g * D_HID + i * P, g * D_HID + (i + 1) * P)
+                hc = slice(g * TOK, (g + 1) * TOK)
+                nc.tensor.matmul_mx(
+                    out=state["ps1"][i][:],
+                    lhsT=w1codes[:, wc].bitcast(FP8X4),
+                    lhsT_scale=w1scales[:, wc],
+                    rhs=hcodes[:, hc].bitcast(FP8X4),
+                    rhs_scale=hscales[:, hc],
+                    start=(g == 0),
+                    stop=(g == 1),
                 )
+
+        def op_gelu(i):
+            nc.scalar.activation(
+                out=hidp[:, i, :], in_=state["ps1"][i][:], func=ACT.Gelu, bias=bias[:, 32 + i : 33 + i], scale=1.0
+            )
+
+        def op_tbls():
             warm_s = keep.tile([P, 1], F32, name="warm_s")
             nc.scalar.activation(out=warm_s[:], in_=hidp[:, 3, 0:1], func=ACT.Sigmoid)
 
@@ -182,20 +188,37 @@ def tile_sparseoutputprojection_pb_kernel(tc, hidden_states, logits, W_f1, b_f1,
                 out=hidcodes[:].bitcast(FP8X4), scales=hidscales[:], in_=hidg[:].rearrange("p r t -> p (r t)")
             )
 
-        def op_a(c):
-            grp = ring.tile([P, CH, 4], BF16, tag="w2grp", name="w2grp%d" % c, align_bytes=64)
+        def grp_tile(c):
+            key = "grp%d" % c
+            if key not in state:
+                state[key] = gring.tile([P, CH, 4], BF16, tag="w2grp", name="w2grp%d" % c, align_bytes=64)
+            return state[key]
+
+        def op_av(c):
             src, s0 = w2_src(c)
-            if W2_VEC[c] > 0:
-                regroup(nc.vector.tensor_copy, grp, src, 0, W2_VEC[c], s0)
-            if W2_VEC[c] < CH:
-                regroup(nc.scalar.copy, grp, src, W2_VEC[c], CH, s0)
-            state["grp%d" % c] = grp
+            regroup(nc.vector.tensor_copy, grp_tile(c), src, 0, W2_VEC[c], s0)
+
+        def op_as(c):
+            src, s0 = w2_src(c)
+            regroup(nc.scalar.copy, grp_tile(c), src, W2_VEC[c], CH - W2_GPS[c], s0)
+
+        def op_ag(c):
+            src, s0 = w2_src(c)
+            c0 = CH - W2_GPS[c]
+            nc.gpsimd.tensor_scalar(
+                out=grp_tile(c)[:, c0:CH, :],
+                in0=src[:, :, s0 + c0 : s0 + CH].rearrange("p t c -> p c t"),
+                scalar1=1.0,
+                scalar2=0.0,
+                op0=ALU.mult,
+                op1=ALU.add,
+            )
 
         def op_b(c):
             nc.vector.quantize_mx(
                 out=w2codes[c][:].bitcast(FP8X4),
                 scales=w2scales[c][:],
-                in_=state["grp%d" % c][:].rearrange("p v t -> p (v t)"),
+                in_=grp_tile(c)[:].rearrange("p v t -> p (v t)"),
             )
 
         def op_c(c):
@@ -225,103 +248,162 @@ def tile_sparseoutputprojection_pb_kernel(tc, hidden_states, logits, W_f1, b_f1,
                 )
             state["sT%d" % c] = st
 
-        def op_e(c):
-            fts = []
-            for a in range(2):
-                ft = psum.tile([P, CH], F32, tag="ft", name="ft%d_%d" % (c, a))
-                for j in range(4):
-                    nc.tensor.transpose(ft[:, j * P : (j + 1) * P], state["sT%d" % c][:, j, a * P : (a + 1) * P], ident[:])
-                fts.append(ft)
-            state["ft%d" % c] = fts
+        def op_e(c, a):
+            ft = psum.tile([P, CH], F32, tag="ft", name="ft%d_%d" % (c, a))
+            for j in range(4):
+                nc.tensor.transpose(ft[:, j * P : (j + 1) * P], state["sT%d" % c][:, j, a * P : (a + 1) * P], ident[:])
+            state["ft%d_%d" % (c, a)] = ft
 
-        def op_f(c):
+        def op_f(c, a):
             lg, l0 = lg_src(c)
-            for a in range(2):
-                nc.vector.scalar_tensor_tensor(
-                    out=osb[c][:, a, :],
-                    in0=state["ft%d" % c][a][:],
-                    scalar=1.0,
-                    in1=lg[:, a, l0 : l0 + CH],
-                    op0=ALU.add,
-                    op1=ALU.mult,
-                )
-                if c == NCH - 1:
-                    nc.sync.dma_start(out=out_dram[:, a, c * CH : (c + 1) * CH], in_=osb[c][:, a, :])
-            if c < NCH - 1:
-                nc.sync.dma_start(out=out_dram[:, :, c * CH : (c + 1) * CH], in_=osb[c][:])
+            nc.vector.scalar_tensor_tensor(
+                out=osb[c][:, a, :],
+                in0=state["ft%d_%d" % (c, a)][:],
+                scalar=1.0,
+                in1=lg[:, a, l0 : l0 + CH],
+                op0=ALU.add,
+                op1=ALU.mult,
+            )
 
-        named = {
-            "bias": op_bias, "bcopy": op_bcopy, "Th": op_th, "evh": op_evh, "qh": op_qh,
-            "MX1": op_mx1, "gelu": op_gelu, "hidre": op_hidre, "qhid": op_qhid,
+        def op_st(c):
+            nc.sync.dma_start(out=out_dram[:, :, c * CH : (c + 1) * CH], in_=osb[c][:])
+
+        def op_sth(c, a):
+            nc.sync.dma_start(out=out_dram[:, a, c * CH : (c + 1) * CH], in_=osb[c][:, a, :])
+
+        ops = {
+            "bcast": (op_bcast, ()), "T_b": (op_tb, ()), "bcopy": (op_bcopy, ()), "q_h": (op_qh, ()),
+            "tblS": (op_tbls, ()), "hidre": (op_hidre, ()), "q_hid": (op_qhid, ()),
         }
-        indexed = {"a": op_a1, "q": op_q1, "A": op_a, "B": op_b, "C": op_c, "D": op_d, "E": op_e, "F": op_f}
+        for g in range(2):
+            ops["T_h%d" % g] = (op_th, (g,))
+            ops["ev_h%d" % g] = (op_evh, (g,))
+            ops["A1V%d" % g] = (op_a1v, (g,))
+            ops["A1S%d" % g] = (op_a1s, (g,))
+            ops["q_w1_%d" % g] = (op_q1, (g,))
+            ops["MX1_%d" % g] = (op_mx1, (g,))
+        for i in range(4):
+            ops["gelu%d" % i] = (op_gelu, (i,))
+        for c in range(NCH):
+            ops["AV%d" % c] = (op_av, (c,))
+            ops["AS%d" % c] = (op_as, (c,))
+            ops["AG%d" % c] = (op_ag, (c,))
+            ops["B%d" % c] = (op_b, (c,))
+            ops["C%d" % c] = (op_c, (c,))
+            ops["D%d" % c] = (op_d, (c,))
+            ops["st%d" % c] = (op_st, (c,))
+            for a in range(2):
+                ops["E%d%s" % (c, "ab"[a])] = (op_e, (c, a))
+                ops["F%d%s" % (c, "ab"[a])] = (op_f, (c, a))
+                ops["st%d%s" % (c, "ab"[a])] = (op_sth, (c, a))
         for word in SEQ:
-            if word in named:
-                named[word]()
-            else:
-                indexed[word[0]](int(word[1:]))
+            fn, args = ops[word]
+            fn(*args)
 
 
 SEQ = (
-    "bias",
-    "a0",
-    "Th",
-    "evh",
-    "q0",
-    "a1",
+    "T_h0",
+    "T_h1",
+    "ev_h0",
+    "A1S0",
+    "A1V0",
+    "ev_h1",
+    "q_w1_0",
+    "A1S1",
+    "q_h",
+    "A1V1",
+    "MX1_0",
+    "bcast",
+    "q_w1_1",
+    "T_b",
+    "AS0",
+    "AV0",
+    "MX1_1",
+    "AS1",
     "bcopy",
-    "qh",
-    "q1",
-    "MX1",
-    "A0",
-    "A1",
+    "AV1",
+    "gelu0",
     "B0",
-    "gelu",
-    "A2",
+    "gelu1",
     "B1",
+    "gelu2",
+    "gelu3",
+    "AS2",
     "hidre",
-    "A3",
-    "qhid",
-    "B2",
+    "q_hid",
+    "tblS",
+    "AV2",
     "C0",
+    "AV3",
     "C1",
     "D0",
-    "E0",
-    "A4",
+    "B2",
+    "AS3",
+    "E0a",
+    "AV4",
+    "E0b",
+    "D1",
     "B3",
     "C2",
-    "D1",
-    "E1",
-    "F0",
-    "A5",
-    "B4",
-    "C3",
+    "F0a",
+    "AS4",
+    "E1a",
+    "F0b",
+    "E1b",
+    "AV5",
     "D2",
-    "E2",
-    "F1",
-    "A6",
-    "B5",
-    "C4",
+    "st0",
+    "C3",
+    "B4",
+    "AS5",
+    "F1a",
+    "E2a",
+    "E2b",
+    "F1b",
     "D3",
-    "E3",
-    "F2",
-    "A7",
-    "B6",
-    "C5",
+    "C4",
+    "AV6",
+    "st1",
+    "B5",
+    "AS6",
+    "E3a",
+    "F2a",
+    "E3b",
     "D4",
-    "E4",
-    "F3",
-    "B7",
-    "C6",
+    "C5",
+    "F2b",
+    "AV7",
+    "st2",
+    "AS7",
+    "E4a",
+    "B6",
+    "E4b",
     "D5",
-    "E5",
-    "F4",
-    "C7",
+    "F3a",
+    "C6",
+    "F3b",
+    "E5a",
+    "B7",
+    "st3",
     "D6",
-    "E6",
-    "F5",
+    "E5b",
+    "F4a",
+    "C7",
+    "F4b",
+    "E6a",
+    "F5a",
+    "st4",
     "D7",
-    "E7",
-    "F6",
-    "F7",
+    "E6b",
+    "F5b",
+    "F6a",
+    "st5",
+    "E7a",
+    "F6b",
+    "E7b",
+    "F7a",
+    "st6",
+    "F7b",
+    "st7a",
+    "st7b",
 )

@@ -13,27 +13,32 @@ ACT = mybir.ActivationFunctionType
 ALU = mybir.AluOpType
 
 P = 128
-TOK = 256
+PACK = 4
+TOKENS = 256
+TOKEN_TILES = TOKENS // P
 D_IN = 1024
+PASSES_1 = D_IN // (P * PACK)
 D_HID = 512
-VOC = 4096
-CH = 512
-NCH = VOC // CH
-FLOPS = 2 * TOK * D_IN * D_HID + 2 * TOK * D_HID * VOC
+HID_TILES = D_HID // P
+VOCAB = 4096
+CHUNK = 512
+CHUNKS = VOCAB // CHUNK
+CHUNK_TILES = CHUNK // P
+BIAS_COLS = VOCAB // P + HID_TILES
 
-W1_VEC = [320,320]
-W2_VEC = [336,336,336,336,336,336,336,336]
-W2_GPS = [0,0,0,0,0,0,0,0]
-W2_LOADS = [[0,2],[2,4],[4,6],[6,8]]
-LG_LOADS = [[0,4],[4,8]]
-LOAD_ORDER = ["h0","g0","g1","w0","w1","l0","w2","w3","l1"]
-GRP_BUFS = 3
+FLOPS = 2 * TOKENS * D_IN * D_HID + 2 * TOKENS * D_HID * VOCAB
+
+W1_VECTOR_COLS = 320
+W2_VECTOR_COLS = 336
+
+W2_LOAD_CHUNKS = 2
+LOGITS_LOAD_CHUNKS = 4
 
 
-def regroup(engine_copy, dst, src, c0, c1, s0):
-    engine_copy(
-        out=dst[:, c0:c1, :].rearrange("p (c i) t -> p c t i", i=4),
-        in_=src[:, :, s0 + c0 : s0 + c1].rearrange("p t (c i) -> p c t i", i=4),
+def regroup(copy, grouped, planes, first, last, offset):
+    copy(
+        out=grouped[:, first:last, :].rearrange("p (c i) t -> p c t i", i=4),
+        in_=planes[:, :, offset + first : offset + last].rearrange("p t (c i) -> p c t i", i=4),
     )
 
 
@@ -43,367 +48,245 @@ def tile_sparseoutputprojection_pb_kernel(tc, hidden_states, logits, W_f1, b_f1,
         ctx.enter_context(tc.manual_schedule())
         keep = ctx.enter_context(tc.tile_pool(name="keep", bufs=1))
         ring = ctx.enter_context(tc.tile_pool(name="ring", bufs=3))
-        gring = ctx.enter_context(tc.tile_pool(name="gring", bufs=GRP_BUFS))
         psum = ctx.enter_context(tc.psum_pool(name="psum", bufs=4))
 
         h_dram = hidden_states.flatten_outer_dims().rearrange("(a p) k -> p a k", p=P)
-        lg_dram = logits.flatten_outer_dims().rearrange("(a p) v -> p a v", p=P)
+        logits_dram = logits.flatten_outer_dims().rearrange("(a p) v -> p a v", p=P)
         out_dram = out.flatten_outer_dims().rearrange("(a p) v -> p a v", p=P)
         w2_dram = W_f2.rearrange("(t p) v -> p t v", p=P)
 
-        braw = keep.tile([P, P], BF16, name="braw")
-        nc.vector.memset(braw[:].bitcast(I32), 0)
-        warm = keep.tile([P, 1], F32, name="warm")
-        nc.vector.memset(warm[:], 0.0)
-        ident = keep.tile([P, P], F32, name="ident")
-        make_identity(nc, ident[:])
-        nc.scalar.dma_start(out=braw[0:32, :], in_=b_f2.rearrange("(j p) -> j p", p=P))
-        nc.scalar.dma_start(out=braw[32:36, :], in_=b_f1.rearrange("(j p) -> j p", p=P))
-        warm_g = keep.tile([P, 1], F32, name="warm_g")
-        nc.scalar.activation(out=warm_g[:], in_=warm[:], func=ACT.Gelu)
+        bias_rows = keep.tile([P, P], BF16, name="bias_rows")
+        nc.vector.memset(bias_rows[:].bitcast(I32), 0)
+        zero = keep.tile([P, 1], F32, name="zero")
+        nc.vector.memset(zero[:], 0.0)
+        identity = keep.tile([P, P], F32, name="identity")
+        make_identity(nc, identity[:])
+        nc.scalar.dma_start(out=bias_rows[0 : VOCAB // P, :], in_=b_f2.rearrange("(j p) -> j p", p=P))
+        nc.scalar.dma_start(out=bias_rows[VOCAB // P : BIAS_COLS, :], in_=b_f1.rearrange("(j p) -> j p", p=P))
+        gelu_warm = keep.tile([P, 1], F32, name="gelu_warm")
+        nc.scalar.activation(out=gelu_warm[:], in_=zero[:], func=ACT.Gelu)
 
-        h_sb = keep.tile([P, 2, D_IN], BF16, name="h_sb")
-        w1raw = [keep.tile([P, 4, D_HID], BF16, name="w1raw%d" % g) for g in range(2)]
-        w2raw = [keep.tile([P, 4, (b - a) * CH], BF16, name="w2raw%d" % i) for i, (a, b) in enumerate(W2_LOADS)]
-        lg_sb = [keep.tile([P, 2, (b - a) * CH], BF16, name="lg%d" % i) for i, (a, b) in enumerate(LG_LOADS)]
-        for item in LOAD_ORDER:
-            kind, idx = item[0], int(item[1:])
-            if kind == "h":
-                nc.sync.dma_start(out=h_sb[:], in_=h_dram)
-            elif kind == "g":
-                nc.sync.dma_start(
-                    out=w1raw[idx][:].rearrange("p (u e) f -> p u e f", u=2),
-                    in_=W_f1[idx * 512 : (idx + 1) * 512, :].rearrange("(u p e) f -> p u e f", u=2, p=P, e=2),
-                )
-            elif kind == "w":
-                a, b = W2_LOADS[idx]
-                nc.sync.dma_start(out=w2raw[idx][:], in_=w2_dram[:, :, a * CH : b * CH])
-            else:
-                a, b = LG_LOADS[idx]
-                nc.sync.dma_start(out=lg_sb[idx][:], in_=lg_dram[:, :, a * CH : b * CH])
-
-        def w2_src(c):
-            for i, (a, b) in enumerate(W2_LOADS):
-                if a <= c < b:
-                    return w2raw[i], (c - a) * CH
-            raise ValueError("chunk")
-
-        def lg_src(c):
-            for i, (a, b) in enumerate(LG_LOADS):
-                if a <= c < b:
-                    return lg_sb[i], (c - a) * CH
-            raise ValueError("chunk")
-
-        bf32 = keep.tile([P, P], F32, name="bf32")
-        bias = keep.tile([P, 36], F32, name="bias")
-        hgrp = keep.tile([P, 2 * TOK * 4], BF16, name="hgrp", align_bytes=64)
-        hcodes = keep.tile([P, 2 * TOK], U32, name="hcodes", align_bytes=64)
-        hscales = keep.tile([P, 2 * TOK], U8, name="hscales", align_bytes=64)
-        w1grp = [keep.tile([P, D_HID, 4], BF16, name="w1grp%d" % g, align_bytes=64) for g in range(2)]
-        w1codes = keep.tile([P, 2 * D_HID], U32, name="w1codes", align_bytes=64)
-        w1scales = keep.tile([P, 2 * D_HID], U8, name="w1scales", align_bytes=64)
-        hidp = keep.tile([P, 4, TOK], BF16, name="hidp")
-        hidg = keep.tile([P, TOK, 4], BF16, name="hidg", align_bytes=64)
-        hidcodes = keep.tile([P, TOK], U32, name="hidcodes", align_bytes=64)
-        hidscales = keep.tile([P, TOK], U8, name="hidscales", align_bytes=64)
-        w2codes = [keep.tile([P, CH], U32, name="w2codes%d" % c, align_bytes=64) for c in range(NCH)]
-        w2scales = [keep.tile([P, CH], U8, name="w2scales%d" % c, align_bytes=64) for c in range(NCH)]
-        osb = [keep.tile([P, 2, CH], F32, name="osb%d" % c) for c in range(NCH)]
-        state = {}
-
-        def op_bcast():
-            nc.vector.tensor_copy(out=bf32[:], in_=braw[:])
-
-        def op_tb():
-            bt = psum.tile([P, P], F32, tag="ft", name="bt")
-            nc.tensor.transpose(bt[:], bf32[:], ident[:])
-            state["bt"] = bt
-
-        def op_bcopy():
-            nc.vector.tensor_copy(out=bias[:], in_=state["bt"][:, 0:36])
-
-        def op_th(g):
-            hw = h_sb[:].rearrange("p a k -> p (a k)").bitcast(F32)
-            xt = psum.tile([P, 2, TOK], F32, tag="ft", name="xt%d" % g)
-            for u in range(2):
-                for a in range(2):
-                    w0 = a * 512 + (2 * g + u) * P
-                    nc.tensor.transpose(xt[:, u, a * P : (a + 1) * P], hw[:, w0 : w0 + P], ident[:])
-            state["xt%d" % g] = xt
-
-        def op_evh(g):
-            copy = nc.vector.tensor_copy if g == 0 else nc.scalar.copy
-            copy(
-                out=hgrp[:].bitcast(F32)[:, g * 512 : (g + 1) * 512].rearrange("p (r u) -> p r u", u=2),
-                in_=state["xt%d" % g][:].rearrange("p u r -> p r u"),
+        h_sb = keep.tile([P, TOKEN_TILES, D_IN], BF16, name="h_sb")
+        nc.sync.dma_start(out=h_sb[:], in_=h_dram)
+        w1_planes = []
+        for g in range(PASSES_1):
+            planes = keep.tile([P, PACK, D_HID], BF16, name="w1_planes%d" % g)
+            nc.sync.dma_start(
+                out=planes[:].rearrange("p (u e) f -> p u e f", u=2),
+                in_=W_f1[g * P * PACK : (g + 1) * P * PACK, :].rearrange("(u p e) f -> p u e f", u=2, p=P, e=2),
             )
+            w1_planes.append(planes)
+        w2_planes = [
+            keep.tile([P, PACK, W2_LOAD_CHUNKS * CHUNK], BF16, name="w2_planes%d" % i)
+            for i in range(CHUNKS // W2_LOAD_CHUNKS)
+        ]
+        logits_sb = [
+            keep.tile([P, TOKEN_TILES, LOGITS_LOAD_CHUNKS * CHUNK], BF16, name="logits_sb%d" % i)
+            for i in range(CHUNKS // LOGITS_LOAD_CHUNKS)
+        ]
 
-        def op_a1v(g):
-            regroup(nc.vector.tensor_copy, w1grp[g], w1raw[g], 0, W1_VEC[g], 0)
+        def load_w2(i):
+            cols = slice(i * W2_LOAD_CHUNKS * CHUNK, (i + 1) * W2_LOAD_CHUNKS * CHUNK)
+            nc.sync.dma_start(out=w2_planes[i][:], in_=w2_dram[:, :, cols])
 
-        def op_a1s(g):
-            regroup(nc.scalar.copy, w1grp[g], w1raw[g], W1_VEC[g], D_HID, 0)
+        def load_logits(i):
+            cols = slice(i * LOGITS_LOAD_CHUNKS * CHUNK, (i + 1) * LOGITS_LOAD_CHUNKS * CHUNK)
+            nc.sync.dma_start(out=logits_sb[i][:], in_=logits_dram[:, :, cols])
 
-        def op_qh():
-            nc.vector.quantize_mx(out=hcodes[:].bitcast(FP8X4), scales=hscales[:], in_=hgrp[:])
+        load_w2(0)
+        load_w2(1)
+        load_w2(2)
+        load_logits(0)
+        load_w2(3)
+        load_logits(1)
 
-        def op_q1(g):
+        bias_f32 = keep.tile([P, P], F32, name="bias_f32")
+        bias = keep.tile([P, BIAS_COLS], F32, name="bias")
+        h_grouped = keep.tile([P, PASSES_1 * TOKENS * PACK], BF16, name="h_grouped", align_bytes=64)
+        h_words = keep.tile([P, PASSES_1 * TOKENS], U32, name="h_words", align_bytes=64)
+        h_scales = keep.tile([P, PASSES_1 * TOKENS], U8, name="h_scales", align_bytes=64)
+        w1_grouped = [
+            keep.tile([P, D_HID, PACK], BF16, name="w1_grouped%d" % g, align_bytes=64) for g in range(PASSES_1)
+        ]
+        w1_words = keep.tile([P, PASSES_1 * D_HID], U32, name="w1_words", align_bytes=64)
+        w1_scales = keep.tile([P, PASSES_1 * D_HID], U8, name="w1_scales", align_bytes=64)
+        hid_planes = keep.tile([P, PACK, TOKENS], BF16, name="hid_planes")
+        hid_grouped = keep.tile([P, TOKENS, PACK], BF16, name="hid_grouped", align_bytes=64)
+        hid_words = keep.tile([P, TOKENS], U32, name="hid_words", align_bytes=64)
+        hid_scales = keep.tile([P, TOKENS], U8, name="hid_scales", align_bytes=64)
+
+        def quantise_w1(g):
             cols = slice(g * D_HID, (g + 1) * D_HID)
             nc.vector.quantize_mx(
-                out=w1codes[:, cols].bitcast(FP8X4),
-                scales=w1scales[:, cols],
-                in_=w1grp[g][:].rearrange("p f t -> p (f t)"),
+                out=w1_words[:, cols].bitcast(FP8X4),
+                scales=w1_scales[:, cols],
+                in_=w1_grouped[g][:].rearrange("p f t -> p (f t)"),
             )
 
-        def op_mx1(g):
-            if g == 0:
-                state["ps1"] = [psum.tile([P, TOK], F32, tag="z", name="ps1_%d" % i) for i in range(4)]
-            for i in range(4):
-                wc = slice(g * D_HID + i * P, g * D_HID + (i + 1) * P)
-                hc = slice(g * TOK, (g + 1) * TOK)
+        def first_matmul(g, products):
+            for i in range(HID_TILES):
+                w_cols = slice(g * D_HID + i * P, g * D_HID + (i + 1) * P)
+                h_cols = slice(g * TOKENS, (g + 1) * TOKENS)
                 nc.tensor.matmul_mx(
-                    out=state["ps1"][i][:],
-                    lhsT=w1codes[:, wc].bitcast(FP8X4),
-                    lhsT_scale=w1scales[:, wc],
-                    rhs=hcodes[:, hc].bitcast(FP8X4),
-                    rhs_scale=hscales[:, hc],
+                    out=products[i][:],
+                    lhsT=w1_words[:, w_cols].bitcast(FP8X4),
+                    lhsT_scale=w1_scales[:, w_cols],
+                    rhs=h_words[:, h_cols].bitcast(FP8X4),
+                    rhs_scale=h_scales[:, h_cols],
                     start=(g == 0),
-                    stop=(g == 1),
+                    stop=(g == PASSES_1 - 1),
                 )
 
-        def op_gelu(i):
-            nc.scalar.activation(
-                out=hidp[:, i, :], in_=state["ps1"][i][:], func=ACT.Gelu, bias=bias[:, 32 + i : 33 + i], scale=1.0
-            )
+        w2_words = [keep.tile([P, CHUNK], U32, name="w2_words%d" % c, align_bytes=64) for c in range(CHUNKS)]
+        w2_scales = [keep.tile([P, CHUNK], U8, name="w2_scales%d" % c, align_bytes=64) for c in range(CHUNKS)]
+        out_sb = [keep.tile([P, TOKEN_TILES, CHUNK], F32, name="out_sb%d" % c) for c in range(CHUNKS)]
+        w2_grouped = {}
+        pre_gate = {}
+        gate_t = {}
+        gate = {}
 
-        def op_tbls():
-            warm_s = keep.tile([P, 1], F32, name="warm_s")
-            nc.scalar.activation(out=warm_s[:], in_=hidp[:, 3, 0:1], func=ACT.Sigmoid)
+        def regroup_w2(c, copy, first, last):
+            if c not in w2_grouped:
+                w2_grouped[c] = ring.tile(
+                    [P, CHUNK, PACK], BF16, tag="w2_grouped", name="w2_grouped%d" % c, align_bytes=64
+                )
+            regroup(copy, w2_grouped[c], w2_planes[c // W2_LOAD_CHUNKS], first, last, (c % W2_LOAD_CHUNKS) * CHUNK)
 
-        def op_hidre():
-            regroup(nc.vector.tensor_copy, hidg, hidp, 0, TOK, 0)
+        def regroup_w2_vector(c):
+            regroup_w2(c, nc.vector.tensor_copy, 0, W2_VECTOR_COLS)
 
-        def op_qhid():
+        def regroup_w2_scalar(c):
+            regroup_w2(c, nc.scalar.copy, W2_VECTOR_COLS, CHUNK)
+
+        def quantise_w2(c):
             nc.vector.quantize_mx(
-                out=hidcodes[:].bitcast(FP8X4), scales=hidscales[:], in_=hidg[:].rearrange("p r t -> p (r t)")
+                out=w2_words[c][:].bitcast(FP8X4),
+                scales=w2_scales[c][:],
+                in_=w2_grouped[c][:].rearrange("p v t -> p (v t)"),
             )
 
-        def grp_tile(c):
-            key = "grp%d" % c
-            if key not in state:
-                state[key] = gring.tile([P, CH, 4], BF16, tag="w2grp", name="w2grp%d" % c, align_bytes=64)
-            return state[key]
-
-        def op_av(c):
-            src, s0 = w2_src(c)
-            regroup(nc.vector.tensor_copy, grp_tile(c), src, 0, W2_VEC[c], s0)
-
-        def op_as(c):
-            src, s0 = w2_src(c)
-            regroup(nc.scalar.copy, grp_tile(c), src, W2_VEC[c], CH - W2_GPS[c], s0)
-
-        def op_ag(c):
-            src, s0 = w2_src(c)
-            c0 = CH - W2_GPS[c]
-            nc.gpsimd.tensor_scalar(
-                out=grp_tile(c)[:, c0:CH, :],
-                in0=src[:, :, s0 + c0 : s0 + CH].rearrange("p t c -> p c t"),
-                scalar1=1.0,
-                scalar2=0.0,
-                op0=ALU.mult,
-                op1=ALU.add,
-            )
-
-        def op_b(c):
-            nc.vector.quantize_mx(
-                out=w2codes[c][:].bitcast(FP8X4),
-                scales=w2scales[c][:],
-                in_=grp_tile(c)[:].rearrange("p v t -> p (v t)"),
-            )
-
-        def op_c(c):
-            zs = [psum.tile([P, 2, TOK], F32, tag="z", name="z%d_%d" % (c, k)) for k in range(2)]
-            for j in range(4):
+        def second_matmul(c):
+            pre_gate[c] = [psum.tile([P, 2, TOKENS], F32, tag="mx", name="pre_gate%d_%d" % (c, b)) for b in range(2)]
+            for j in range(CHUNK_TILES):
                 cols = slice(j * P, (j + 1) * P)
                 nc.tensor.matmul_mx(
-                    out=zs[j // 2][:, j % 2, :],
-                    lhsT=w2codes[c][:, cols].bitcast(FP8X4),
-                    lhsT_scale=w2scales[c][:, cols],
-                    rhs=hidcodes[:].bitcast(FP8X4),
-                    rhs_scale=hidscales[:],
+                    out=pre_gate[c][j // 2][:, j % 2, :],
+                    lhsT=w2_words[c][:, cols].bitcast(FP8X4),
+                    lhsT_scale=w2_scales[c][:, cols],
+                    rhs=hid_words[:].bitcast(FP8X4),
+                    rhs_scale=hid_scales[:],
                     start=True,
                     stop=True,
                 )
-            state["z%d" % c] = zs
 
-        def op_d(c):
-            st = ring.tile([P, 4, TOK], F32, tag="sT", name="sT%d" % c)
-            for j in range(4):
+        def sigmoid(c):
+            gate_t[c] = ring.tile([P, CHUNK_TILES, TOKENS], F32, tag="gate_t", name="gate_t%d" % c)
+            for j in range(CHUNK_TILES):
+                col = c * CHUNK_TILES + j
                 nc.scalar.activation(
-                    out=st[:, j, :],
-                    in_=state["z%d" % c][j // 2][:, j % 2, :],
+                    out=gate_t[c][:, j, :],
+                    in_=pre_gate[c][j // 2][:, j % 2, :],
                     func=ACT.Sigmoid,
-                    bias=bias[:, 4 * c + j : 4 * c + j + 1],
+                    bias=bias[:, col : col + 1],
                     scale=1.0,
                 )
-            state["sT%d" % c] = st
 
-        def op_e(c, a):
-            ft = psum.tile([P, CH], F32, tag="ft", name="ft%d_%d" % (c, a))
-            for j in range(4):
-                nc.tensor.transpose(ft[:, j * P : (j + 1) * P], state["sT%d" % c][:, j, a * P : (a + 1) * P], ident[:])
-            state["ft%d_%d" % (c, a)] = ft
+        def transpose_gate(c):
+            for a in range(TOKEN_TILES):
+                gate[c, a] = psum.tile([P, CHUNK], F32, tag="tr", name="gate%d_%d" % (c, a))
+                for j in range(CHUNK_TILES):
+                    nc.tensor.transpose(
+                        gate[c, a][:, j * P : (j + 1) * P], gate_t[c][:, j, a * P : (a + 1) * P], identity[:]
+                    )
 
-        def op_f(c, a):
-            lg, l0 = lg_src(c)
-            nc.vector.scalar_tensor_tensor(
-                out=osb[c][:, a, :],
-                in0=state["ft%d_%d" % (c, a)][:],
-                scalar=1.0,
-                in1=lg[:, a, l0 : l0 + CH],
-                op0=ALU.add,
-                op1=ALU.mult,
+        def multiply_and_store(c):
+            first = (c % LOGITS_LOAD_CHUNKS) * CHUNK
+            cols = slice(c * CHUNK, (c + 1) * CHUNK)
+            for a in range(TOKEN_TILES):
+                nc.vector.scalar_tensor_tensor(
+                    out=out_sb[c][:, a, :],
+                    in0=gate[c, a][:],
+                    scalar=1.0,
+                    in1=logits_sb[c // LOGITS_LOAD_CHUNKS][:, a, first : first + CHUNK],
+                    op0=ALU.add,
+                    op1=ALU.mult,
+                )
+            if c < CHUNKS - 1:
+                nc.sync.dma_start(out=out_dram[:, :, cols], in_=out_sb[c][:])
+            else:
+                for a in range(TOKEN_TILES):
+                    nc.sync.dma_start(out=out_dram[:, a, cols], in_=out_sb[c][:, a, :])
+
+        h_as_words = h_sb[:].rearrange("p a k -> p (a k)").bitcast(F32)
+        h_t = []
+        for g in range(PASSES_1):
+            bank = psum.tile([P, 2, TOKENS], F32, tag="tr", name="h_t%d" % g)
+            for u in range(2):
+                for a in range(TOKEN_TILES):
+                    first = a * (D_IN // 2) + (2 * g + u) * P
+                    nc.tensor.transpose(bank[:, u, a * P : (a + 1) * P], h_as_words[:, first : first + P], identity[:])
+            h_t.append(bank)
+
+        def evacuate_h(g, copy):
+            words = slice(g * TOKENS * 2, (g + 1) * TOKENS * 2)
+            copy(
+                out=h_grouped[:].bitcast(F32)[:, words].rearrange("p (r u) -> p r u", u=2),
+                in_=h_t[g][:].rearrange("p u r -> p r u"),
             )
 
-        def op_st(c):
-            nc.sync.dma_start(out=out_dram[:, :, c * CH : (c + 1) * CH], in_=osb[c][:])
+        evacuate_h(0, nc.vector.tensor_copy)
+        regroup(nc.scalar.copy, w1_grouped[0], w1_planes[0], W1_VECTOR_COLS, D_HID, 0)
+        regroup(nc.vector.tensor_copy, w1_grouped[0], w1_planes[0], 0, W1_VECTOR_COLS, 0)
+        evacuate_h(1, nc.scalar.copy)
+        quantise_w1(0)
+        regroup(nc.scalar.copy, w1_grouped[1], w1_planes[1], W1_VECTOR_COLS, D_HID, 0)
+        nc.vector.quantize_mx(out=h_words[:].bitcast(FP8X4), scales=h_scales[:], in_=h_grouped[:])
+        regroup(nc.vector.tensor_copy, w1_grouped[1], w1_planes[1], 0, W1_VECTOR_COLS, 0)
+        hid_pre = [psum.tile([P, TOKENS], F32, tag="mx", name="hid_pre%d" % i) for i in range(HID_TILES)]
+        first_matmul(0, hid_pre)
+        nc.vector.tensor_copy(out=bias_f32[:], in_=bias_rows[:])
+        quantise_w1(1)
+        bias_t = psum.tile([P, P], F32, tag="tr", name="bias_t")
+        nc.tensor.transpose(bias_t[:], bias_f32[:], identity[:])
+        first_matmul(1, hid_pre)
 
-        def op_sth(c, a):
-            nc.sync.dma_start(out=out_dram[:, a, c * CH : (c + 1) * CH], in_=osb[c][:, a, :])
+        regroup_w2_vector(0)
+        regroup_w2_scalar(0)
+        regroup_w2_scalar(1)
+        nc.vector.tensor_copy(out=bias[:], in_=bias_t[:, 0:BIAS_COLS])
+        regroup_w2_vector(1)
+        for i in range(HID_TILES):
+            nc.scalar.activation(
+                out=hid_planes[:, i, :],
+                in_=hid_pre[i][:],
+                func=ACT.Gelu,
+                bias=bias[:, VOCAB // P + i : VOCAB // P + i + 1],
+                scale=1.0,
+            )
+        quantise_w2(0)
+        quantise_w2(1)
+        regroup_w2_scalar(2)
+        regroup(nc.vector.tensor_copy, hid_grouped, hid_planes, 0, TOKENS, 0)
+        sigmoid_warm = keep.tile([P, 1], F32, name="sigmoid_warm")
+        nc.scalar.activation(out=sigmoid_warm[:], in_=hid_planes[:, HID_TILES - 1, 0:1], func=ACT.Sigmoid)
+        nc.vector.quantize_mx(
+            out=hid_words[:].bitcast(FP8X4), scales=hid_scales[:], in_=hid_grouped[:].rearrange("p r t -> p (r t)")
+        )
+        regroup_w2_vector(2)
+        regroup_w2_vector(3)
+        quantise_w2(2)
+        second_matmul(0)
+        second_matmul(1)
 
-        ops = {
-            "bcast": (op_bcast, ()), "T_b": (op_tb, ()), "bcopy": (op_bcopy, ()), "q_h": (op_qh, ()),
-            "tblS": (op_tbls, ()), "hidre": (op_hidre, ()), "q_hid": (op_qhid, ()),
-        }
-        for g in range(2):
-            ops["T_h%d" % g] = (op_th, (g,))
-            ops["ev_h%d" % g] = (op_evh, (g,))
-            ops["A1V%d" % g] = (op_a1v, (g,))
-            ops["A1S%d" % g] = (op_a1s, (g,))
-            ops["q_w1_%d" % g] = (op_q1, (g,))
-            ops["MX1_%d" % g] = (op_mx1, (g,))
-        for i in range(4):
-            ops["gelu%d" % i] = (op_gelu, (i,))
-        for c in range(NCH):
-            ops["AV%d" % c] = (op_av, (c,))
-            ops["AS%d" % c] = (op_as, (c,))
-            ops["AG%d" % c] = (op_ag, (c,))
-            ops["B%d" % c] = (op_b, (c,))
-            ops["C%d" % c] = (op_c, (c,))
-            ops["D%d" % c] = (op_d, (c,))
-            ops["st%d" % c] = (op_st, (c,))
-            for a in range(2):
-                ops["E%d%s" % (c, "ab"[a])] = (op_e, (c, a))
-                ops["F%d%s" % (c, "ab"[a])] = (op_f, (c, a))
-                ops["st%d%s" % (c, "ab"[a])] = (op_sth, (c, a))
-        for word in SEQ:
-            fn, args = ops[word]
-            fn(*args)
-
-
-SEQ = (
-    "T_h0",
-    "T_h1",
-    "ev_h0",
-    "A1S0",
-    "A1V0",
-    "ev_h1",
-    "q_w1_0",
-    "A1S1",
-    "q_h",
-    "A1V1",
-    "MX1_0",
-    "bcast",
-    "q_w1_1",
-    "T_b",
-    "AS0",
-    "AV0",
-    "MX1_1",
-    "AS1",
-    "bcopy",
-    "AV1",
-    "gelu0",
-    "B0",
-    "gelu1",
-    "B1",
-    "gelu2",
-    "gelu3",
-    "AS2",
-    "hidre",
-    "q_hid",
-    "tblS",
-    "AV2",
-    "C0",
-    "AV3",
-    "C1",
-    "D0",
-    "B2",
-    "AS3",
-    "E0a",
-    "AV4",
-    "E0b",
-    "D1",
-    "B3",
-    "C2",
-    "F0a",
-    "AS4",
-    "E1a",
-    "F0b",
-    "E1b",
-    "AV5",
-    "D2",
-    "st0",
-    "C3",
-    "B4",
-    "AS5",
-    "F1a",
-    "E2a",
-    "E2b",
-    "F1b",
-    "D3",
-    "C4",
-    "AV6",
-    "st1",
-    "B5",
-    "AS6",
-    "E3a",
-    "F2a",
-    "E3b",
-    "D4",
-    "C5",
-    "F2b",
-    "AV7",
-    "st2",
-    "AS7",
-    "E4a",
-    "B6",
-    "E4b",
-    "D5",
-    "F3a",
-    "C6",
-    "F3b",
-    "E5a",
-    "B7",
-    "st3",
-    "D6",
-    "E5b",
-    "F4a",
-    "C7",
-    "F4b",
-    "E6a",
-    "F5a",
-    "st4",
-    "D7",
-    "E6b",
-    "F5b",
-    "F6a",
-    "st5",
-    "E7a",
-    "F6b",
-    "E7b",
-    "F7a",
-    "st6",
-    "F7b",
-    "st7a",
-    "st7b",
-)
+        for c in range(CHUNKS):
+            sigmoid(c)
+            if c + 3 < CHUNKS:
+                regroup_w2_scalar(c + 3)
+            transpose_gate(c)
+            if c + 2 < CHUNKS:
+                second_matmul(c + 2)
+            if c + 4 < CHUNKS:
+                regroup_w2_vector(c + 4)
+            if c + 3 < CHUNKS:
+                quantise_w2(c + 3)
+            multiply_and_store(c)

@@ -67,7 +67,6 @@ def tile_sparseoutputprojection_pb_kernel(tc, hidden_states, logits, W_f1, b_f1,
         nc.scalar.activation(out=gelu_warm[:], in_=zero[:], func=ACT.Gelu)
 
         h_sb = keep.tile([P, TOKEN_TILES, D_IN], BF16, name="h_sb")
-        nc.sync.dma_start(out=h_sb[:], in_=h_dram)
         w1_planes = []
         for g in range(PASSES_1):
             planes = keep.tile([P, PACK, D_HID], BF16, name="w1_planes%d" % g)
@@ -76,6 +75,8 @@ def tile_sparseoutputprojection_pb_kernel(tc, hidden_states, logits, W_f1, b_f1,
                 in_=W_f1[g * P * PACK : (g + 1) * P * PACK, :].rearrange("(u p e) f -> p u e f", u=2, p=P, e=2),
             )
             w1_planes.append(planes)
+            if g == 0:
+                nc.sync.dma_start(out=h_sb[:], in_=h_dram)
         w2_planes = [
             keep.tile([P, PACK, W2_LOAD_CHUNKS * CHUNK], BF16, name="w2_planes%d" % i)
             for i in range(CHUNKS // W2_LOAD_CHUNKS)
@@ -234,14 +235,14 @@ def tile_sparseoutputprojection_pb_kernel(tc, hidden_states, logits, W_f1, b_f1,
                 in_=h_t[g][:].rearrange("p u r -> p r u"),
             )
 
-        evacuate_h(0, nc.vector.tensor_copy)
         regroup(nc.scalar.copy, w1_grouped[0], w1_planes[0], W1_VECTOR_COLS, D_HID, 0)
         regroup(nc.vector.tensor_copy, w1_grouped[0], w1_planes[0], 0, W1_VECTOR_COLS, 0)
-        evacuate_h(1, nc.scalar.copy)
         quantise_w1(0)
+        evacuate_h(0, nc.vector.tensor_copy)
+        evacuate_h(1, nc.scalar.copy)
         regroup(nc.scalar.copy, w1_grouped[1], w1_planes[1], W1_VECTOR_COLS, D_HID, 0)
-        nc.vector.quantize_mx(out=h_words[:].bitcast(FP8X4), scales=h_scales[:], in_=h_grouped[:])
         regroup(nc.vector.tensor_copy, w1_grouped[1], w1_planes[1], 0, W1_VECTOR_COLS, 0)
+        nc.vector.quantize_mx(out=h_words[:].bitcast(FP8X4), scales=h_scales[:], in_=h_grouped[:])
         hid_pre = [psum.tile([P, TOKENS], F32, tag="mx", name="hid_pre%d" % i) for i in range(HID_TILES)]
         first_matmul(0, hid_pre)
         nc.vector.tensor_copy(out=bias_f32[:], in_=bias_rows[:])

@@ -31,6 +31,9 @@ FLOPS = 2 * TOKENS * D_IN * D_HID + 2 * TOKENS * D_HID * VOCAB
 W1_VECTOR_COLS = 320
 W2_VECTOR_COLS = 336
 
+ORDER = (0, 1, 2, 3, 4, 6, 7, 5)
+SINGLE = 3
+
 W2_LOAD_CHUNKS = 2
 LOGITS_LOAD_CHUNKS = 4
 
@@ -148,10 +151,16 @@ def tile_sparseoutputprojection_pb_kernel(tc, hidden_states, logits, W_f1, b_f1,
 
         def regroup_w2(c, copy, first, last):
             if c not in w2_grouped:
-                w2_grouped[c] = ring.tile(
-                    [P, CHUNK, PACK], BF16, tag="w2_grouped", name="w2_grouped%d" % c, align_bytes=64
-                )
-            regroup(copy, w2_grouped[c], w2_planes[c // W2_LOAD_CHUNKS], first, last, (c % W2_LOAD_CHUNKS) * CHUNK)
+                if c == SINGLE:
+                    w2_grouped[c] = keep.tile(
+                        [P, CHUNK, PACK], BF16, tag="single", name="w2_grouped%d" % c, align_bytes=64
+                    )
+                else:
+                    w2_grouped[c] = ring.tile(
+                        [P, CHUNK, PACK], BF16, tag="w2_grouped", name="w2_grouped%d" % c, align_bytes=64
+                    )
+            load, place = divmod(ORDER[c], W2_LOAD_CHUNKS)
+            regroup(copy, w2_grouped[c], w2_planes[load], first, last, place * CHUNK)
 
         def regroup_w2_vector(c):
             regroup_w2(c, nc.vector.tensor_copy, 0, W2_VECTOR_COLS)
@@ -164,6 +173,29 @@ def tile_sparseoutputprojection_pb_kernel(tc, hidden_states, logits, W_f1, b_f1,
                 out=w2_words[c][:].bitcast(FP8X4),
                 scales=w2_scales[c][:],
                 in_=w2_grouped[c][:].rearrange("p v t -> p (v t)"),
+            )
+
+        gpsimd_grouped = {}
+
+        def regroup_gpsimd(j):
+            gpsimd_grouped[j] = keep.tile([P, P, PACK], BF16, tag="single", name="gpsimd_grouped%d" % j, align_bytes=64)
+            load, place = divmod(ORDER[CHUNKS - 1], W2_LOAD_CHUNKS)
+            first = place * CHUNK + j * P
+            nc.gpsimd.tensor_scalar(
+                out=gpsimd_grouped[j][:],
+                in0=w2_planes[load][:, :, first : first + P].rearrange("p t c -> p c t"),
+                scalar1=1.0,
+                scalar2=0.0,
+                op0=ALU.mult,
+                op1=ALU.add,
+            )
+
+        def quantise_gpsimd(j):
+            cols = slice(j * P, (j + 1) * P)
+            nc.vector.quantize_mx(
+                out=w2_words[CHUNKS - 1][:, cols].bitcast(FP8X4),
+                scales=w2_scales[CHUNKS - 1][:, cols],
+                in_=gpsimd_grouped[j][:].rearrange("p v t -> p (v t)"),
             )
 
         def second_matmul(c):
@@ -183,7 +215,7 @@ def tile_sparseoutputprojection_pb_kernel(tc, hidden_states, logits, W_f1, b_f1,
         def sigmoid(c):
             gate_t[c] = ring.tile([P, CHUNK_TILES, TOKENS], F32, tag="gate_t", name="gate_t%d" % c)
             for j in range(CHUNK_TILES):
-                col = c * CHUNK_TILES + j
+                col = ORDER[c] * CHUNK_TILES + j
                 nc.scalar.activation(
                     out=gate_t[c][:, j, :],
                     in_=pre_gate[c][j // 2][:, j % 2, :],
@@ -201,14 +233,15 @@ def tile_sparseoutputprojection_pb_kernel(tc, hidden_states, logits, W_f1, b_f1,
                     )
 
         def multiply_and_store(c):
-            first = (c % LOGITS_LOAD_CHUNKS) * CHUNK
-            cols = slice(c * CHUNK, (c + 1) * CHUNK)
+            load, place = divmod(ORDER[c], LOGITS_LOAD_CHUNKS)
+            first = place * CHUNK
+            cols = slice(ORDER[c] * CHUNK, (ORDER[c] + 1) * CHUNK)
             for a in range(TOKEN_TILES):
                 nc.vector.scalar_tensor_tensor(
                     out=out_sb[c][:, a, :],
                     in0=gate[c, a][:],
                     scalar=1.0,
-                    in1=logits_sb[c // LOGITS_LOAD_CHUNKS][:, a, first : first + CHUNK],
+                    in1=logits_sb[load][:, a, first : first + CHUNK],
                     op0=ALU.add,
                     op1=ALU.mult,
                 )
@@ -281,13 +314,17 @@ def tile_sparseoutputprojection_pb_kernel(tc, hidden_states, logits, W_f1, b_f1,
 
         for c in range(CHUNKS):
             sigmoid(c)
-            if c + 3 < CHUNKS:
+            if c + 3 < CHUNKS - 1:
                 regroup_w2_scalar(c + 3)
             transpose_gate(c)
             if c + 2 < CHUNKS:
                 second_matmul(c + 2)
-            if c + 4 < CHUNKS:
+            if c + 4 < CHUNKS - 1:
                 regroup_w2_vector(c + 4)
-            if c + 3 < CHUNKS:
+            if c + 3 < CHUNKS - 1:
                 quantise_w2(c + 3)
+            if 1 <= c <= CHUNK_TILES:
+                quantise_gpsimd(c - 1)
+            if c < CHUNK_TILES:
+                regroup_gpsimd(c)
             multiply_and_store(c)

@@ -245,11 +245,7 @@ def tile_sparseoutputprojection_pb_kernel(tc, hidden_states, logits, W_f1, b_f1,
                     op0=ALU.add,
                     op1=ALU.mult,
                 )
-            if c < CHUNKS - 1:
-                nc.sync.dma_start(out=out_dram[:, :, cols], in_=out_sb[c][:])
-            else:
-                for a in range(TOKEN_TILES):
-                    nc.sync.dma_start(out=out_dram[:, a, cols], in_=out_sb[c][:, a, :])
+                nc.sync.dma_start(out=out_dram[:, a, cols], in_=out_sb[c][:, a, :])
 
         h_as_words = h_sb[:].rearrange("p a k -> p (a k)").bitcast(F32)
         h_t = []

@@ -34,14 +34,14 @@ W2_VECTOR_COLS = 336
 ORDER = (0, 1, 2, 3, 4, 6, 7, 5)
 SINGLE = 3
 
-W2_LOAD_CHUNKS = 2
-LOGITS_LOAD_CHUNKS = 4
+W2_LOADS = ((0,), (1,), (2, 3), (4, 5), (6, 7))
+LOGITS_LOADS = ((0, 1), (2, 3), (4, 5, 6, 7))
 
 
-def regroup(copy, grouped, planes, first, last, offset):
+def regroup(copy, grouped, planes, first, last):
     copy(
         out=grouped[:, first:last, :].rearrange("p (c i) t -> p c t i", i=4),
-        in_=planes[:, :, offset + first : offset + last].rearrange("p t (c i) -> p c t i", i=4),
+        in_=planes[:, :, first:last].rearrange("p t (c i) -> p c t i", i=4),
     )
 
 
@@ -80,29 +80,29 @@ def tile_sparseoutputprojection_pb_kernel(tc, hidden_states, logits, W_f1, b_f1,
             w1_planes.append(planes)
             if g == 0:
                 nc.sync.dma_start(out=h_sb[:], in_=h_dram)
-        w2_planes = [
-            keep.tile([P, PACK, W2_LOAD_CHUNKS * CHUNK], BF16, name="w2_planes%d" % i)
-            for i in range(CHUNKS // W2_LOAD_CHUNKS)
-        ]
-        logits_sb = [
-            keep.tile([P, TOKEN_TILES, LOGITS_LOAD_CHUNKS * CHUNK], BF16, name="logits_sb%d" % i)
-            for i in range(CHUNKS // LOGITS_LOAD_CHUNKS)
-        ]
+        w2_planes = {}
+        logits_sb = {}
+
+        def load(parts, dram, chunks, middle, name):
+            tile = keep.tile([P, middle, len(chunks) * CHUNK], BF16, name=name)
+            nc.sync.dma_start(out=tile[:], in_=dram[:, :, chunks[0] * CHUNK : (chunks[-1] + 1) * CHUNK])
+            for i, chunk in enumerate(chunks):
+                parts[chunk] = tile[:, :, i * CHUNK : (i + 1) * CHUNK]
 
         def load_w2(i):
-            cols = slice(i * W2_LOAD_CHUNKS * CHUNK, (i + 1) * W2_LOAD_CHUNKS * CHUNK)
-            nc.sync.dma_start(out=w2_planes[i][:], in_=w2_dram[:, :, cols])
+            load(w2_planes, w2_dram, W2_LOADS[i], PACK, "w2_planes%d" % i)
 
         def load_logits(i):
-            cols = slice(i * LOGITS_LOAD_CHUNKS * CHUNK, (i + 1) * LOGITS_LOAD_CHUNKS * CHUNK)
-            nc.sync.dma_start(out=logits_sb[i][:], in_=logits_dram[:, :, cols])
+            load(logits_sb, logits_dram, LOGITS_LOADS[i], TOKEN_TILES, "logits_sb%d" % i)
 
         load_w2(0)
         load_w2(1)
         load_w2(2)
-        load_logits(0)
         load_w2(3)
+        load_logits(0)
+        load_w2(4)
         load_logits(1)
+        load_logits(2)
 
         bias_f32 = keep.tile([P, P], F32, name="bias_f32")
         bias = keep.tile([P, BIAS_COLS], F32, name="bias")
@@ -159,8 +159,7 @@ def tile_sparseoutputprojection_pb_kernel(tc, hidden_states, logits, W_f1, b_f1,
                     w2_grouped[c] = ring.tile(
                         [P, CHUNK, PACK], BF16, tag="w2_grouped", name="w2_grouped%d" % c, align_bytes=64
                     )
-            load, place = divmod(ORDER[c], W2_LOAD_CHUNKS)
-            regroup(copy, w2_grouped[c], w2_planes[load], first, last, place * CHUNK)
+            regroup(copy, w2_grouped[c], w2_planes[ORDER[c]], first, last)
 
         def regroup_w2_vector(c):
             regroup_w2(c, nc.vector.tensor_copy, 0, W2_VECTOR_COLS)
@@ -179,11 +178,10 @@ def tile_sparseoutputprojection_pb_kernel(tc, hidden_states, logits, W_f1, b_f1,
 
         def regroup_gpsimd(j):
             gpsimd_grouped[j] = keep.tile([P, P, PACK], BF16, tag="single", name="gpsimd_grouped%d" % j, align_bytes=64)
-            load, place = divmod(ORDER[CHUNKS - 1], W2_LOAD_CHUNKS)
-            first = place * CHUNK + j * P
+            first = j * P
             nc.gpsimd.tensor_scalar(
                 out=gpsimd_grouped[j][:],
-                in0=w2_planes[load][:, :, first : first + P].rearrange("p t c -> p c t"),
+                in0=w2_planes[ORDER[CHUNKS - 1]][:, :, first : first + P].rearrange("p t c -> p c t"),
                 scalar1=1.0,
                 scalar2=0.0,
                 op0=ALU.mult,
@@ -233,15 +231,13 @@ def tile_sparseoutputprojection_pb_kernel(tc, hidden_states, logits, W_f1, b_f1,
                     )
 
         def multiply_and_store(c):
-            load, place = divmod(ORDER[c], LOGITS_LOAD_CHUNKS)
-            first = place * CHUNK
             cols = slice(ORDER[c] * CHUNK, (ORDER[c] + 1) * CHUNK)
             for a in range(TOKEN_TILES):
                 nc.vector.scalar_tensor_tensor(
                     out=out_sb[c][:, a, :],
                     in0=gate[c, a][:],
                     scalar=1.0,
-                    in1=logits_sb[load][:, a, first : first + CHUNK],
+                    in1=logits_sb[ORDER[c]][:, a, :],
                     op0=ALU.add,
                     op1=ALU.mult,
                 )
@@ -264,13 +260,13 @@ def tile_sparseoutputprojection_pb_kernel(tc, hidden_states, logits, W_f1, b_f1,
                 in_=h_t[g][:].rearrange("p u r -> p r u"),
             )
 
-        regroup(nc.scalar.copy, w1_grouped[0], w1_planes[0], W1_VECTOR_COLS, D_HID, 0)
-        regroup(nc.vector.tensor_copy, w1_grouped[0], w1_planes[0], 0, W1_VECTOR_COLS, 0)
+        regroup(nc.scalar.copy, w1_grouped[0], w1_planes[0], W1_VECTOR_COLS, D_HID)
+        regroup(nc.vector.tensor_copy, w1_grouped[0], w1_planes[0], 0, W1_VECTOR_COLS)
         quantise_w1(0)
         evacuate_h(0, nc.vector.tensor_copy)
         evacuate_h(1, nc.scalar.copy)
-        regroup(nc.scalar.copy, w1_grouped[1], w1_planes[1], W1_VECTOR_COLS, D_HID, 0)
-        regroup(nc.vector.tensor_copy, w1_grouped[1], w1_planes[1], 0, W1_VECTOR_COLS, 0)
+        regroup(nc.scalar.copy, w1_grouped[1], w1_planes[1], W1_VECTOR_COLS, D_HID)
+        regroup(nc.vector.tensor_copy, w1_grouped[1], w1_planes[1], 0, W1_VECTOR_COLS)
         nc.vector.quantize_mx(out=h_words[:].bitcast(FP8X4), scales=h_scales[:], in_=h_grouped[:])
         hid_pre = [psum.tile([P, TOKENS], F32, tag="mx", name="hid_pre%d" % i) for i in range(HID_TILES)]
         first_matmul(0, hid_pre)
@@ -296,7 +292,7 @@ def tile_sparseoutputprojection_pb_kernel(tc, hidden_states, logits, W_f1, b_f1,
         quantise_w2(0)
         quantise_w2(1)
         regroup_w2_scalar(2)
-        regroup(nc.vector.tensor_copy, hid_grouped, hid_planes, 0, TOKENS, 0)
+        regroup(nc.vector.tensor_copy, hid_grouped, hid_planes, 0, TOKENS)
         sigmoid_warm = keep.tile([P, 1], F32, name="sigmoid_warm")
         nc.scalar.activation(out=sigmoid_warm[:], in_=hid_planes[:, HID_TILES - 1, 0:1], func=ACT.Sigmoid)
         nc.vector.quantize_mx(

@@ -28,7 +28,7 @@ BIAS_COLS = VOCAB // P + HID_TILES
 
 FLOPS = 2 * TOKENS * D_IN * D_HID + 2 * TOKENS * D_HID * VOCAB
 
-W1_VECTOR_COLS = 320
+W1_VECTOR_COLS = 352
 W2_VECTOR_COLS = 336
 
 ORDER = (0, 1, 2, 3, 4, 6, 7, 5)
@@ -58,12 +58,14 @@ def tile_sparseoutputprojection_pb_kernel(tc, hidden_states, logits, W_f1, b_f1,
         out_dram = out.flatten_outer_dims().rearrange("(a p) v -> p a v", p=P)
         w2_dram = W_f2.rearrange("(t p) v -> p t v", p=P)
 
+        identity_bf16 = keep.tile([P, P], BF16, name="identity_bf16")
         bias_rows = keep.tile([P, P], BF16, name="bias_rows")
         nc.vector.memset(bias_rows[:].bitcast(I32), 0)
         zero = keep.tile([P, 1], F32, name="zero")
         nc.vector.memset(zero[:], 0.0)
         identity = keep.tile([P, P], F32, name="identity")
         make_identity(nc, identity[:])
+        make_identity(nc, identity_bf16[:])
         nc.scalar.dma_start(out=bias_rows[0 : VOCAB // P, :], in_=b_f2.rearrange("(j p) -> j p", p=P))
         nc.scalar.dma_start(out=bias_rows[VOCAB // P : BIAS_COLS, :], in_=b_f1.rearrange("(j p) -> j p", p=P))
         gelu_warm = keep.tile([P, 1], F32, name="gelu_warm")
@@ -104,7 +106,6 @@ def tile_sparseoutputprojection_pb_kernel(tc, hidden_states, logits, W_f1, b_f1,
         load_logits(1)
         load_logits(2)
 
-        bias_f32 = keep.tile([P, P], F32, name="bias_f32")
         bias = keep.tile([P, BIAS_COLS], F32, name="bias")
         h_grouped = keep.tile([P, PASSES_1 * TOKENS * PACK], BF16, name="h_grouped", align_bytes=64)
         h_words = keep.tile([P, PASSES_1 * TOKENS], U32, name="h_words", align_bytes=64)
@@ -253,6 +254,9 @@ def tile_sparseoutputprojection_pb_kernel(tc, hidden_states, logits, W_f1, b_f1,
                     nc.tensor.transpose(bank[:, u, a * P : (a + 1) * P], h_as_words[:, first : first + P], identity[:])
             h_t.append(bank)
 
+        bias_t = psum.tile([P, P], BF16, tag="tr", name="bias_t")
+        nc.tensor.transpose(bias_t[:], bias_rows[:], identity_bf16[:])
+
         def evacuate_h(g, copy):
             words = slice(g * TOKENS * 2, (g + 1) * TOKENS * 2)
             copy(
@@ -270,16 +274,13 @@ def tile_sparseoutputprojection_pb_kernel(tc, hidden_states, logits, W_f1, b_f1,
         nc.vector.quantize_mx(out=h_words[:].bitcast(FP8X4), scales=h_scales[:], in_=h_grouped[:])
         hid_pre = [psum.tile([P, TOKENS], F32, tag="mx", name="hid_pre%d" % i) for i in range(HID_TILES)]
         first_matmul(0, hid_pre)
-        nc.vector.tensor_copy(out=bias_f32[:], in_=bias_rows[:])
         quantise_w1(1)
-        bias_t = psum.tile([P, P], F32, tag="tr", name="bias_t")
-        nc.tensor.transpose(bias_t[:], bias_f32[:], identity[:])
         first_matmul(1, hid_pre)
 
+        nc.scalar.copy(out=bias[:], in_=bias_t[:, 0:BIAS_COLS])
         regroup_w2_vector(0)
         regroup_w2_scalar(0)
         regroup_w2_scalar(1)
-        nc.vector.tensor_copy(out=bias[:], in_=bias_t[:, 0:BIAS_COLS])
         regroup_w2_vector(1)
         for i in range(HID_TILES):
             nc.scalar.activation(
@@ -289,12 +290,12 @@ def tile_sparseoutputprojection_pb_kernel(tc, hidden_states, logits, W_f1, b_f1,
                 bias=bias[:, VOCAB // P + i : VOCAB // P + i + 1],
                 scale=1.0,
             )
+        sigmoid_warm = keep.tile([P, 1], F32, name="sigmoid_warm")
+        nc.scalar.activation(out=sigmoid_warm[:], in_=hid_planes[:, HID_TILES - 1, 0:1], func=ACT.Sigmoid)
         quantise_w2(0)
         quantise_w2(1)
         regroup_w2_scalar(2)
         regroup(nc.vector.tensor_copy, hid_grouped, hid_planes, 0, TOKENS)
-        sigmoid_warm = keep.tile([P, 1], F32, name="sigmoid_warm")
-        nc.scalar.activation(out=sigmoid_warm[:], in_=hid_planes[:, HID_TILES - 1, 0:1], func=ACT.Sigmoid)
         nc.vector.quantize_mx(
             out=hid_words[:].bitcast(FP8X4), scales=hid_scales[:], in_=hid_grouped[:].rearrange("p r t -> p (r t)")
         )
@@ -303,11 +304,12 @@ def tile_sparseoutputprojection_pb_kernel(tc, hidden_states, logits, W_f1, b_f1,
         quantise_w2(2)
         second_matmul(0)
         second_matmul(1)
+        regroup_w2_scalar(3)
 
         for c in range(CHUNKS):
             sigmoid(c)
-            if c + 3 < CHUNKS - 1:
-                regroup_w2_scalar(c + 3)
+            if c + 4 < CHUNKS - 1:
+                regroup_w2_scalar(c + 4)
             transpose_gate(c)
             if c + 2 < CHUNKS:
                 second_matmul(c + 2)

from contextlib import ExitStack

import concourse.mybir as mybir
from concourse.masks import make_identity

F32 = mybir.dt.float32
BF16 = mybir.dt.bfloat16
I32 = mybir.dt.int32
U32 = mybir.dt.uint32
U8 = mybir.dt.uint8
FP8X4 = mybir.dt.float8_e4m3fn_x4
ACT = mybir.ActivationFunctionType
ALU = mybir.AluOpType

P = 128
PACK = 4
TOKENS = 256
TOKEN_TILES = TOKENS // P
D_IN = 1024
PASSES_1 = D_IN // (P * PACK)
D_HID = 512
HID_TILES = D_HID // P
VOCAB = 4096
CHUNK = 512
CHUNKS = VOCAB // CHUNK
CHUNK_TILES = CHUNK // P
BIAS_COLS = VOCAB // P + HID_TILES

FLOPS = 2 * TOKENS * D_IN * D_HID + 2 * TOKENS * D_HID * VOCAB

W1_VECTOR_COLS = 352
W2_VECTOR_COLS = 336

ORDER = (0, 1, 2, 3, 4, 6, 7, 5)
SINGLE = 3

W2_LOADS = ((0,), (1,), (2, 3), (4, 5), (6, 7))
LOGITS_LOADS = ((0, 1), (2, 3), (4, 5, 6, 7))


def regroup(copy, grouped, planes, first, last):
    copy(
        out=grouped[:, first:last, :].rearrange("p (c i) t -> p c t i", i=4),
        in_=planes[:, :, first:last].rearrange("p t (c i) -> p c t i", i=4),
    )


def tile_sparseoutputprojection_pb_kernel(tc, hidden_states, logits, W_f1, b_f1, W_f2, b_f2, out):
    nc = tc.nc
    with ExitStack() as ctx:
        ctx.enter_context(tc.manual_schedule())
        keep = ctx.enter_context(tc.tile_pool(name="keep", bufs=1))
        ring = ctx.enter_context(tc.tile_pool(name="ring", bufs=3))
        psum = ctx.enter_context(tc.psum_pool(name="psum", bufs=4))

        h_dram = hidden_states.flatten_outer_dims().rearrange("(a p) k -> p a k", p=P)
        logits_dram = logits.flatten_outer_dims().rearrange("(a p) v -> p a v", p=P)
        out_dram = out.flatten_outer_dims().rearrange("(a p) v -> p a v", p=P)
        w2_dram = W_f2.rearrange("(t p) v -> p t v", p=P)

        identity_bf16 = keep.tile([P, P], BF16, name="identity_bf16")
        bias_rows = keep.tile([P, P], BF16, name="bias_rows")
        nc.vector.memset(bias_rows[:].bitcast(I32), 0)
        zero = keep.tile([P, 1], F32, name="zero")
        nc.vector.memset(zero[:], 0.0)
        identity = keep.tile([P, P], F32, name="identity")
        make_identity(nc, identity[:])
        make_identity(nc, identity_bf16[:])
        nc.scalar.dma_start(out=bias_rows[0 : VOCAB // P, :], in_=b_f2.rearrange("(j p) -> j p", p=P))
        nc.scalar.dma_start(out=bias_rows[VOCAB // P : BIAS_COLS, :], in_=b_f1.rearrange("(j p) -> j p", p=P))
        gelu_warm = keep.tile([P, 1], F32, name="gelu_warm")
        nc.scalar.activation(out=gelu_warm[:], in_=zero[:], func=ACT.Gelu)

        h_sb = keep.tile([P, TOKEN_TILES, D_IN], BF16, name="h_sb")
        w1_planes = []
        for g in range(PASSES_1):
            planes = keep.tile([P, PACK, D_HID], BF16, name="w1_planes%d" % g)
            nc.sync.dma_start(
                out=planes[:].rearrange("p (u e) f -> p u e f", u=2),
                in_=W_f1[g * P * PACK : (g + 1) * P * PACK, :].rearrange("(u p e) f -> p u e f", u=2, p=P, e=2),
            )
            w1_planes.append(planes)
            if g == 0:
                nc.sync.dma_start(out=h_sb[:], in_=h_dram)
        w2_planes = {}
        logits_sb = {}

        def load(parts, dram, chunks, middle, name):
            tile = keep.tile([P, middle, len(chunks) * CHUNK], BF16, name=name)
            nc.sync.dma_start(out=tile[:], in_=dram[:, :, chunks[0] * CHUNK : (chunks[-1] + 1) * CHUNK])
            for i, chunk in enumerate(chunks):
                parts[chunk] = tile[:, :, i * CHUNK : (i + 1) * CHUNK]

        def load_w2(i):
            load(w2_planes, w2_dram, W2_LOADS[i], PACK, "w2_planes%d" % i)

        def load_logits(i):
            load(logits_sb, logits_dram, LOGITS_LOADS[i], TOKEN_TILES, "logits_sb%d" % i)

        load_w2(0)
        load_w2(1)
        load_w2(2)
        load_w2(3)
        load_logits(0)
        load_w2(4)
        load_logits(1)
        load_logits(2)

        bias = keep.tile([P, BIAS_COLS], F32, name="bias")
        h_grouped = keep.tile([P, PASSES_1 * TOKENS * PACK], BF16, name="h_grouped", align_bytes=64)
        h_words = keep.tile([P, PASSES_1 * TOKENS], U32, name="h_words", align_bytes=64)
        h_scales = keep.tile([P, PASSES_1 * TOKENS], U8, name="h_scales", align_bytes=64)
        w1_grouped = [
            keep.tile([P, D_HID, PACK], BF16, name="w1_grouped%d" % g, align_bytes=64) for g in range(PASSES_1)
        ]
        w1_words = keep.tile([P, PASSES_1 * D_HID], U32, name="w1_words", align_bytes=64)
        w1_scales = keep.tile([P, PASSES_1 * D_HID], U8, name="w1_scales", align_bytes=64)
        hid_planes = keep.tile([P, PACK, TOKENS], BF16, name="hid_planes")
        hid_grouped = keep.tile([P, TOKENS, PACK], BF16, name="hid_grouped", align_bytes=64)
        hid_words = keep.tile([P, TOKENS], U32, name="hid_words", align_bytes=64)
        hid_scales = keep.tile([P, TOKENS], U8, name="hid_scales", align_bytes=64)

        def quantise_w1(g):
            cols = slice(g * D_HID, (g + 1) * D_HID)
            nc.vector.quantize_mx(
                out=w1_words[:, cols].bitcast(FP8X4),
                scales=w1_scales[:, cols],
                in_=w1_grouped[g][:].rearrange("p f t -> p (f t)"),
            )

        def first_matmul(g, products):
            for i in range(HID_TILES):
                w_cols = slice(g * D_HID + i * P, g * D_HID + (i + 1) * P)
                h_cols = slice(g * TOKENS, (g + 1) * TOKENS)
                nc.tensor.matmul_mx(
                    out=products[i][:],
                    lhsT=w1_words[:, w_cols].bitcast(FP8X4),
                    lhsT_scale=w1_scales[:, w_cols],
                    rhs=h_words[:, h_cols].bitcast(FP8X4),
                    rhs_scale=h_scales[:, h_cols],
                    start=(g == 0),
                    stop=(g == PASSES_1 - 1),
                )

        w2_words = [keep.tile([P, CHUNK], U32, name="w2_words%d" % c, align_bytes=64) for c in range(CHUNKS)]
        w2_scales = [keep.tile([P, CHUNK], U8, name="w2_scales%d" % c, align_bytes=64) for c in range(CHUNKS)]
        out_sb = [keep.tile([P, TOKEN_TILES, CHUNK], F32, name="out_sb%d" % c) for c in range(CHUNKS)]
        w2_grouped = {}
        pre_gate = {}
        gate_t = {}
        gate = {}

        def regroup_w2(c, copy, first, last):
            if c not in w2_grouped:
                if c == SINGLE:
                    w2_grouped[c] = keep.tile(
                        [P, CHUNK, PACK], BF16, tag="single", name="w2_grouped%d" % c, align_bytes=64
                    )
                else:
                    w2_grouped[c] = ring.tile(
                        [P, CHUNK, PACK], BF16, tag="w2_grouped", name="w2_grouped%d" % c, align_bytes=64
                    )
            regroup(copy, w2_grouped[c], w2_planes[ORDER[c]], first, last)

        def regroup_w2_vector(c):
            regroup_w2(c, nc.vector.tensor_copy, 0, W2_VECTOR_COLS)

        def regroup_w2_scalar(c):
            regroup_w2(c, nc.scalar.copy, W2_VECTOR_COLS, CHUNK)

        def quantise_w2(c):
            nc.vector.quantize_mx(
                out=w2_words[c][:].bitcast(FP8X4),
                scales=w2_scales[c][:],
                in_=w2_grouped[c][:].rearrange("p v t -> p (v t)"),
            )

        gpsimd_grouped = {}

        def regroup_gpsimd(j):
            gpsimd_grouped[j] = keep.tile([P, P, PACK], BF16, tag="single", name="gpsimd_grouped%d" % j, align_bytes=64)
            first = j * P
            nc.gpsimd.tensor_scalar(
                out=gpsimd_grouped[j][:],
                in0=w2_planes[ORDER[CHUNKS - 1]][:, :, first : first + P].rearrange("p t c -> p c t"),
                scalar1=1.0,
                scalar2=0.0,
                op0=ALU.mult,
                op1=ALU.add,
            )

        def quantise_gpsimd(j):
            cols = slice(j * P, (j + 1) * P)
            nc.vector.quantize_mx(
                out=w2_words[CHUNKS - 1][:, cols].bitcast(FP8X4),
                scales=w2_scales[CHUNKS - 1][:, cols],
                in_=gpsimd_grouped[j][:].rearrange("p v t -> p (v t)"),
            )

        def second_matmul(c):
            pre_gate[c] = [psum.tile([P, 2, TOKENS], F32, tag="mx", name="pre_gate%d_%d" % (c, b)) for b in range(2)]
            for j in range(CHUNK_TILES):
                cols = slice(j * P, (j + 1) * P)
                nc.tensor.matmul_mx(
                    out=pre_gate[c][j // 2][:, j % 2, :],
                    lhsT=w2_words[c][:, cols].bitcast(FP8X4),
                    lhsT_scale=w2_scales[c][:, cols],
                    rhs=hid_words[:].bitcast(FP8X4),
                    rhs_scale=hid_scales[:],
                    start=True,
                    stop=True,
                )

        def sigmoid(c):
            gate_t[c] = ring.tile([P, CHUNK_TILES, TOKENS], F32, tag="gate_t", name="gate_t%d" % c)
            for j in range(CHUNK_TILES):
                col = ORDER[c] * CHUNK_TILES + j
                nc.scalar.activation(
                    out=gate_t[c][:, j, :],
                    in_=pre_gate[c][j // 2][:, j % 2, :],
                    func=ACT.Sigmoid,
                    bias=bias[:, col : col + 1],
                    scale=1.0,
                )

        def transpose_gate(c):
            for a in range(TOKEN_TILES):
                gate[c, a] = psum.tile([P, CHUNK], F32, tag="tr", name="gate%d_%d" % (c, a))
                for j in range(CHUNK_TILES):
                    nc.tensor.transpose(
                        gate[c, a][:, j * P : (j + 1) * P], gate_t[c][:, j, a * P : (a + 1) * P], identity[:]
                    )

        def multiply_and_store(c):
            cols = slice(ORDER[c] * CHUNK, (ORDER[c] + 1) * CHUNK)
            for a in range(TOKEN_TILES):
                nc.vector.scalar_tensor_tensor(
                    out=out_sb[c][:, a, :],
                    in0=gate[c, a][:],
                    scalar=1.0,
                    in1=logits_sb[ORDER[c]][:, a, :],
                    op0=ALU.add,
                    op1=ALU.mult,
                )
                nc.sync.dma_start(out=out_dram[:, a, cols], in_=out_sb[c][:, a, :])

        h_as_words = h_sb[:].rearrange("p a k -> p (a k)").bitcast(F32)
        h_t = []
        for g in range(PASSES_1):
            bank = psum.tile([P, 2, TOKENS], F32, tag="tr", name="h_t%d" % g)
            for u in range(2):
                for a in range(TOKEN_TILES):
                    first = a * (D_IN // 2) + (2 * g + u) * P
                    nc.tensor.transpose(bank[:, u, a * P : (a + 1) * P], h_as_words[:, first : first + P], identity[:])
            h_t.append(bank)

        bias_t = psum.tile([P, P], BF16, tag="tr", name="bias_t")
        nc.tensor.transpose(bias_t[:], bias_rows[:], identity_bf16[:])

        def evacuate_h(g, copy):
            words = slice(g * TOKENS * 2, (g + 1) * TOKENS * 2)
            copy(
                out=h_grouped[:].bitcast(F32)[:, words].rearrange("p (r u) -> p r u", u=2),
                in_=h_t[g][:].rearrange("p u r -> p r u"),
            )

        regroup(nc.scalar.copy, w1_grouped[0], w1_planes[0], W1_VECTOR_COLS, D_HID)
        regroup(nc.vector.tensor_copy, w1_grouped[0], w1_planes[0], 0, W1_VECTOR_COLS)
        quantise_w1(0)
        evacuate_h(0, nc.vector.tensor_copy)
        evacuate_h(1, nc.scalar.copy)
        regroup(nc.scalar.copy, w1_grouped[1], w1_planes[1], W1_VECTOR_COLS, D_HID)
        regroup(nc.vector.tensor_copy, w1_grouped[1], w1_planes[1], 0, W1_VECTOR_COLS)
        nc.vector.quantize_mx(out=h_words[:].bitcast(FP8X4), scales=h_scales[:], in_=h_grouped[:])
        hid_pre = [psum.tile([P, TOKENS], F32, tag="mx", name="hid_pre%d" % i) for i in range(HID_TILES)]
        first_matmul(0, hid_pre)
        quantise_w1(1)
        first_matmul(1, hid_pre)

        nc.scalar.copy(out=bias[:], in_=bias_t[:, 0:BIAS_COLS])
        regroup_w2_vector(0)
        regroup_w2_scalar(0)
        regroup_w2_scalar(1)
        regroup_w2_vector(1)
        for i in range(HID_TILES):
            nc.scalar.activation(
                out=hid_planes[:, i, :],
                in_=hid_pre[i][:],
                func=ACT.Gelu,
                bias=bias[:, VOCAB // P + i : VOCAB // P + i + 1],
                scale=1.0,
            )
        sigmoid_warm = keep.tile([P, 1], F32, name="sigmoid_warm")
        nc.scalar.activation(out=sigmoid_warm[:], in_=hid_planes[:, HID_TILES - 1, 0:1], func=ACT.Sigmoid)
        quantise_w2(0)
        quantise_w2(1)
        regroup_w2_scalar(2)
        regroup(nc.vector.tensor_copy, hid_grouped, hid_planes, 0, TOKENS)
        nc.vector.quantize_mx(
            out=hid_words[:].bitcast(FP8X4), scales=hid_scales[:], in_=hid_grouped[:].rearrange("p r t -> p (r t)")
        )
        regroup_w2_vector(2)
        regroup_w2_vector(3)
        quantise_w2(2)
        second_matmul(0)
        second_matmul(1)
        regroup_w2_scalar(3)

        for c in range(CHUNKS):
            sigmoid(c)
            if c + 4 < CHUNKS - 1:
                regroup_w2_scalar(c + 4)
            transpose_gate(c)
            if c + 2 < CHUNKS:
                second_matmul(c + 2)
            if c + 4 < CHUNKS - 1:
                regroup_w2_vector(c + 4)
            if c + 3 < CHUNKS - 1:
                quantise_w2(c + 3)
            if 1 <= c <= CHUNK_TILES:
                quantise_gpsimd(c - 1)
            if c < CHUNK_TILES:
                regroup_gpsimd(c)
            multiply_and_store(c)
